import numpy as np
import ml_dtypes


def mxq(x, axis, fmt="e4m3"):
    dtype, down = {"e4m3": (ml_dtypes.float8_e4m3fn, 7), "e5m2": (ml_dtypes.float8_e5m2, 14)}[fmt]
    v = np.moveaxis(np.asarray(x, np.float32).astype(ml_dtypes.bfloat16).astype(np.float64), axis, -1)
    blocks = v.reshape(v.shape[:-1] + (-1, 32))
    amax = np.abs(blocks).max(-1, keepdims=True)
    byte = np.maximum(np.where(amax > 0, np.frexp(amax)[1] - 1 + 127, 0) - down, 1)
    scale = np.exp2(byte - 127.0)
    codes = (blocks / scale).astype(np.float32).astype(dtype).astype(np.float64)
    return np.moveaxis((codes * scale).reshape(v.shape), -1, axis)


WIDE = False


def mx_kscale(k):
    if not WIDE:
        return np.ones(k)
    levels = np.array([10, -10, 5, -5, 0])
    a = np.random.permutation(np.resize(levels, k // 512 * 4)).reshape(k // 512, 4)
    idx = np.arange(k)
    return np.exp2(a[idx // 512, idx % 128 // 32])


BF16 = ml_dtypes.bfloat16


def bf(x):
    return np.asarray(x, np.float32).astype(BF16)


def f64(x):
    return np.asarray(x).astype(np.float64)


E2M1 = np.array([0.0, 0.5, 1.0, 1.5, 2.0, 3.0, 4.0, 6.0, -0.0, -0.5, -1.0, -1.5, -2.0, -3.0, -4.0, -6.0])


def pack_weight(w, fmt):
    k, n = w.shape
    w = f64(bf(w)).reshape(k // 32, 32, n)
    amax = np.abs(w).max(1)
    if fmt == "e4m3":
        byte = np.frexp(amax)[1] - 1 + 127 - 7
    else:
        mant, ex = np.frexp(amax / 6.0)
        byte = np.where(mant > 0.5, ex, ex - 1) + 127
    byte = np.clip(np.where(amax > 0, byte, 1), 1, 254)
    scaled = (w * np.exp2(127.0 - byte)[:, None, :]).reshape(k, n).astype(np.float32)
    by_word = np.ascontiguousarray(scaled.reshape(k // 512, 128, 4, n).transpose(0, 1, 3, 2))
    if fmt == "e4m3":
        words = by_word.astype(ml_dtypes.float8_e4m3fn).view(np.uint8)
    else:
        c = by_word.astype(ml_dtypes.float4_e2m1fn).view(np.uint8) & 0xF
        words = c[..., 0::2] | (c[..., 1::2] << 4)
    return np.ascontiguousarray(words), np.ascontiguousarray(byte.astype(np.uint8).reshape(k // 512, 16, n))


def unpack_weight(words, scales, fmt):
    g, p, n, _ = words.shape
    if fmt == "e4m3":
        vals = np.ascontiguousarray(words).view(ml_dtypes.float8_e4m3fn).astype(np.float64)
    else:
        nib = np.empty((g, p, n, 4), np.uint8)
        nib[..., 0::2] = words & 0xF
        nib[..., 1::2] = words >> 4
        vals = E2M1[nib]
    vals = vals * np.repeat(np.exp2(scales.astype(np.float64) - 127.0), 8, axis=1)[..., None]
    return vals.transpose(0, 1, 3, 2).reshape(g * 512, n)


B, IN, H = 512, 1024, 1024
QH = H % (16 * 32) == 0
FMT = "e4m3"


def sigmoid(v):
    return 1.0 / (1.0 + np.exp(-v))


def setup_inputs():
    s = mx_kscale(IN)
    one = np.ones(H)
    inp = {"x": bf(np.random.standard_normal((B, IN)) * s), "hidden": bf(np.random.standard_normal((B, H)))}
    for name, fan_in, f in (("Wir", IN, s), ("Whr", H, one), ("Wiz", IN, s), ("Whz", H, one), ("Win", IN, s), ("Whn", H, one)):
        w = np.random.standard_normal((H, fan_in)) / np.sqrt(fan_in) / f[None, :]
        words, scales = pack_weight(np.ascontiguousarray(w.T), FMT)
        inp[name + "_w_words"] = words
        inp[name + "_w_scales"] = scales
        inp[name + "_b"] = bf(np.random.standard_normal(H) * 0.2)
    return inp


def reference(x, hidden, Wir_w_words, Wir_w_scales, Wir_b, Whr_w_words, Whr_w_scales, Whr_b, Wiz_w_words, Wiz_w_scales, Wiz_b, Whz_w_words, Whz_w_scales, Whz_b, Win_w_words, Win_w_scales, Win_b, Whn_w_words, Whn_w_scales, Whn_b):
    x, hidden = f64(x), f64(hidden)
    Wi = np.concatenate([unpack_weight(Wir_w_words, Wir_w_scales, FMT).T, unpack_weight(Wiz_w_words, Wiz_w_scales, FMT).T, unpack_weight(Win_w_words, Win_w_scales, FMT).T], axis=0)
    Wh = np.concatenate([unpack_weight(Whr_w_words, Whr_w_scales, FMT).T, unpack_weight(Whz_w_words, Whz_w_scales, FMT).T, unpack_weight(Whn_w_words, Whn_w_scales, FMT).T], axis=0)
    bi = np.concatenate([f64(Wir_b), f64(Wiz_b), f64(Win_b)], axis=0)
    bh = np.concatenate([f64(Whr_b), f64(Whz_b), f64(Whn_b)], axis=0)
    gi = (mxq(x, 1, "e4m3") @ Wi.T) + bi
    if QH:
        gh = (mxq(hidden, 1, "e4m3") @ Wh.T) + bh
    else:
        gh = hidden @ Wh.T + bh
    ir, iz, inn = np.split(gi, 3, axis=1)
    hr, hz, hn = np.split(gh, 3, axis=1)
    rt = sigmoid(ir + hr)
    zt = sigmoid(iz + hz)
    nt = np.tanh(inn + rt * hn)
    ht = (1.0 - zt) * nt + zt * hidden
    return ht

@@ -1,0 +1,261 @@
+from contextlib import ExitStack
+
+import concourse.mybir as mybir
+from concourse.masks import make_identity
+
+F32 = mybir.dt.float32
+BF16 = mybir.dt.bfloat16
+I32 = mybir.dt.int32
+U32 = mybir.dt.uint32
+U8 = mybir.dt.uint8
+FP8X4 = mybir.dt.float8_e4m3fn_x4
+ACT = mybir.ActivationFunctionType
+ALU = mybir.AluOpType
+
+P = 128
+BATCH = 512
+K = 1024
+FEATURES = 1024
+K_PASS = 4 * P
+PASSES = K // K_PASS
+BATCH_TILES = BATCH // P
+FEATURE_TILES = FEATURES // P
+ROUND_TILES = 2
+ROUNDS = FEATURE_TILES // ROUND_TILES
+ROUND_COLS = ROUND_TILES * P
+
+FLOPS = 2 * BATCH * K * FEATURES * 6
+
+PRODUCTS = (
+    ("r", (("x", "Wir"), ("h", "Whr"))),
+    ("hn", (("h", "Whn"),)),
+    ("in", (("x", "Win"),)),
+    ("z", (("x", "Wiz"), ("h", "Whz"))),
+)
+WEIGHT_ORDER = ("Wir", "Whr", "Whn", "Win", "Wiz", "Whz")
+
+
+def tile_gru_kernel(
+    tc,
+    x,
+    hidden,
+    Wir_w_words,
+    Wir_w_scales,
+    Wir_b,
+    Whr_w_words,
+    Whr_w_scales,
+    Whr_b,
+    Wiz_w_words,
+    Wiz_w_scales,
+    Wiz_b,
+    Whz_w_words,
+    Whz_w_scales,
+    Whz_b,
+    Win_w_words,
+    Win_w_scales,
+    Win_b,
+    Whn_w_words,
+    Whn_w_scales,
+    Whn_b,
+    out,
+):
+    nc = tc.nc
+    dram_words = {"Wir": Wir_w_words, "Whr": Whr_w_words, "Wiz": Wiz_w_words, "Whz": Whz_w_words, "Win": Win_w_words, "Whn": Whn_w_words}
+    dram_scales = {"Wir": Wir_w_scales, "Whr": Whr_w_scales, "Wiz": Wiz_w_scales, "Whz": Whz_w_scales, "Win": Win_w_scales, "Whn": Whn_w_scales}
+    dram_bias = {"Wir": Wir_b, "Whr": Whr_b, "Wiz": Wiz_b, "Whz": Whz_b, "Win": Win_b, "Whn": Whn_b}
+    dram_rows = {"x": x, "h": hidden}
+
+    with ExitStack() as stack:
+        stack.enter_context(tc.manual_schedule())
+        keep = stack.enter_context(tc.tile_pool(name="keep", bufs=1))
+        work = stack.enter_context(tc.tile_pool(name="work", bufs=ROUND_TILES + 1))
+        late = stack.enter_context(tc.tile_pool(name="late", bufs=2 * ROUND_TILES + 1))
+        psum = stack.enter_context(tc.psum_pool(name="psum", bufs=8))
+
+        planes = {}
+        plane_offset = {}
+        for index, name in enumerate(WEIGHT_ORDER):
+            if index % 2 == 0:
+                shared = keep.tile([P, FEATURES], U8, name="planes_%d" % (index // 2), align_bytes=64)
+                nc.vector.memset(shared[:].bitcast(I32), 0)
+            planes[name] = shared
+            plane_offset[name] = 8 * (index % 2)
+        bias_rows = keep.tile([P, P], BF16, name="bias_rows")
+        nc.vector.memset(bias_rows[:], 0.0)
+        zero_col = keep.tile([P, 1], F32, name="zero_col")
+        nc.vector.memset(zero_col[:], 0.0)
+
+        ident_f32 = keep.tile([P, P], F32, name="ident_f32")
+        make_identity(nc, ident_f32[:])
+        ident_bf16 = keep.tile([P, P], BF16, name="ident_bf16")
+        make_identity(nc, ident_bf16[:])
+
+        warm_col = keep.tile([P, 1], F32, name="warm_col")
+        nc.scalar.activation(out=warm_col[:], in_=zero_col[:], func=ACT.Sigmoid)
+
+        for index, name in enumerate(WEIGHT_ORDER):
+            nc.gpsimd.dma_start(
+                out=bias_rows[FEATURE_TILES * index : FEATURE_TILES * (index + 1), :],
+                in_=dram_bias[name].rearrange("(m j) -> m j", j=P),
+            )
+
+        rows = {}
+        for act in ("x", "h"):
+            for bt in range(BATCH_TILES):
+                rows[act, bt] = keep.tile([P, K], BF16, name="rows_%s_%d" % (act, bt))
+                nc.sync.dma_start(out=rows[act, bt][:], in_=dram_rows[act][P * bt : P * (bt + 1), :])
+
+        words = {}
+
+        def load_words(name, rnd):
+            words[name, rnd] = keep.tile([P, PASSES, ROUND_COLS], I32, name="words_%s_%d" % (name, rnd), align_bytes=64)
+            source = dram_words[name].rearrange("g p n t -> p g (n t)")
+            nc.sync.dma_start(
+                out=words[name, rnd][:],
+                in_=source[:, :, 4 * ROUND_COLS * rnd : 4 * ROUND_COLS * (rnd + 1)].bitcast(I32),
+            )
+
+        for name in WEIGHT_ORDER:
+            for quadrant in range(4):
+                first = 32 * quadrant + plane_offset[name]
+                nc.sync.dma_start(
+                    out=planes[name][first : first + 4 * PASSES, :].bitcast(I32),
+                    in_=dram_scales[name][:, 4 * quadrant : 4 * quadrant + 4, :].bitcast(I32),
+                )
+            load_words(name, 0)
+        for rnd in range(1, ROUNDS):
+            for name in WEIGHT_ORDER:
+                load_words(name, rnd)
+
+        grouped = {}
+        codes = {}
+        act_planes = {}
+        for act in ("x", "h"):
+            grouped[act] = keep.tile([P, PASSES, 4 * BATCH], BF16, name="grouped_" + act, align_bytes=64)
+            codes[act] = keep.tile([P, PASSES, BATCH], U32, name="codes_" + act, align_bytes=64)
+            act_planes[act] = keep.tile([P, PASSES, BATCH], U8, name="act_planes_" + act, align_bytes=64)
+
+        def copy_out(index, out_ap, in_ap):
+            if index % 2 == 0:
+                nc.vector.tensor_copy(out=out_ap, in_=in_ap)
+            else:
+                nc.scalar.copy(out=out_ap, in_=in_ap)
+
+        def transpose_pairs(index, act, bt):
+            pairs = rows[act, bt][:].bitcast(F32)
+            bank = psum.tile([P, PASSES, 2, P], F32, name="pairs_T", tag="bank")
+            for g in range(PASSES):
+                for u in range(2):
+                    nc.tensor.transpose(bank[:, g, u, :], pairs[:, 256 * g + u : 256 * (g + 1) : 2], ident_f32[:])
+            target = grouped[act][:].bitcast(F32).rearrange("p g (b u) -> p g b u", u=2)
+            copy_out(index, target[:, :, P * bt : P * (bt + 1), :], bank[:].rearrange("p g u b -> p g b u"))
+
+        def quantise(act, bt):
+            for g in range(PASSES):
+                nc.vector.quantize_mx(
+                    out=codes[act][:, g, P * bt : P * (bt + 1)].bitcast(FP8X4),
+                    scales=act_planes[act][:, g, P * bt : P * (bt + 1)],
+                    in_=grouped[act][:, g, 4 * P * bt : 4 * P * (bt + 1)],
+                )
+
+        row_tiles = [(act, bt) for act in ("x", "h") for bt in range(BATCH_TILES)]
+        for index, (act, bt) in enumerate(row_tiles):
+            transpose_pairs(index, act, bt)
+            if index > 0:
+                quantise(*row_tiles[index - 1])
+        quantise(*row_tiles[-1])
+
+        hidden_T = keep.tile([P, FEATURE_TILES, BATCH], BF16, name="hidden_T")
+        for half in range(FEATURE_TILES // 2):
+            bank = psum.tile([P, 2, BATCH_TILES, P], BF16, name="hidden_T_bank", tag="bank")
+            for i in range(2):
+                m = 2 * half + i
+                for bt in range(BATCH_TILES):
+                    nc.tensor.transpose(bank[:, i, bt, :], rows["h", bt][:, P * m : P * (m + 1)], ident_bf16[:])
+            copy_out(
+                half,
+                hidden_T[:, 2 * half : 2 * half + 2, :].rearrange("p m b -> p (m b)"),
+                bank[:].rearrange("p i t b -> p (i t b)"),
+            )
+
+        bias_bank = psum.tile([P, P], BF16, name="bias_bank", tag="bank")
+        nc.tensor.transpose(bias_bank[:], bias_rows[:], ident_bf16[:])
+        bias_cols = keep.tile([P, len(WEIGHT_ORDER) * FEATURE_TILES], F32, name="bias_cols")
+        nc.vector.tensor_copy(out=bias_cols[:], in_=bias_bank[:, 0 : len(WEIGHT_ORDER) * FEATURE_TILES])
+        bias = {}
+        for index, name in enumerate(WEIGHT_ORDER):
+            bias[name] = bias_cols[:, FEATURE_TILES * index : FEATURE_TILES * (index + 1)]
+        bias_r = keep.tile([P, FEATURE_TILES], F32, name="bias_r")
+        nc.vector.tensor_tensor(out=bias_r[:], in0=bias["Wir"], in1=bias["Whr"], op=ALU.add)
+        bias_z = keep.tile([P, FEATURE_TILES], F32, name="bias_z")
+        nc.vector.tensor_tensor(out=bias_z[:], in0=bias["Wiz"], in1=bias["Whz"], op=ALU.add)
+
+        def multiply(rnd):
+            banks = {}
+            for product, pairs in PRODUCTS:
+                for i in range(ROUND_TILES):
+                    m = ROUND_TILES * rnd + i
+                    bank = psum.tile([P, BATCH], F32, name="bank_" + product, tag="bank")
+                    banks[product, i] = bank
+                    steps = [(act, name, g) for act, name in pairs for g in range(PASSES)]
+                    for step, (act, name, g) in enumerate(steps):
+                        nc.tensor.matmul_mx(
+                            out=bank[:],
+                            lhsT=words[name, rnd][:, g, P * i : P * (i + 1)].bitcast(FP8X4),
+                            lhsT_scale=planes[name][plane_offset[name] + 4 * g : P, P * m : P * (m + 1)],
+                            rhs=codes[act][:, g, :].bitcast(FP8X4),
+                            rhs_scale=act_planes[act][:, g, :],
+                            start=(step == 0),
+                            stop=(step == len(steps) - 1),
+                        )
+            return banks
+
+        def gates(rnd, banks):
+            tiles = range(ROUND_TILES)
+            cols = [slice(ROUND_TILES * rnd + i, ROUND_TILES * rnd + i + 1) for i in tiles]
+            r, rh, pre, n, z, diff, step, res = {}, {}, {}, {}, {}, {}, {}, {}
+            for i in tiles:
+                r[i] = work.tile([P, BATCH], F32, name="r")
+                nc.scalar.activation(out=r[i][:], in_=banks["r", i][:], func=ACT.Sigmoid, bias=bias_r[:, cols[i]])
+            for i in tiles:
+                rh[i] = work.tile([P, BATCH], F32, name="rh")
+                nc.vector.scalar_tensor_tensor(
+                    out=rh[i][:], in0=banks["hn", i][:], scalar=bias["Whn"][:, cols[i]], in1=r[i][:], op0=ALU.add, op1=ALU.mult
+                )
+            for i in tiles:
+                pre[i] = work.tile([P, BATCH], F32, name="pre")
+                nc.vector.tensor_tensor(out=pre[i][:], in0=banks["in", i][:], in1=rh[i][:], op=ALU.add)
+            for i in tiles:
+                n[i] = work.tile([P, BATCH], F32, name="n")
+                nc.scalar.activation(out=n[i][:], in_=pre[i][:], func=ACT.Tanh, bias=bias["Win"][:, cols[i]])
+            for i in tiles:
+                diff[i] = work.tile([P, BATCH], F32, name="diff")
+                nc.vector.tensor_tensor(out=diff[i][:], in0=hidden_T[:, ROUND_TILES * rnd + i, :], in1=n[i][:], op=ALU.subtract)
+            for i in tiles:
+                z[i] = work.tile([P, BATCH], F32, name="z")
+                nc.scalar.activation(out=z[i][:], in_=banks["z", i][:], func=ACT.Sigmoid, bias=bias_z[:, cols[i]])
+            for i in tiles:
+                step[i] = work.tile([P, BATCH], F32, name="step")
+                nc.vector.tensor_tensor(out=step[i][:], in0=z[i][:], in1=diff[i][:], op=ALU.mult)
+                res[i] = late.tile([P, BATCH], F32, name="res")
+                nc.vector.tensor_tensor(out=res[i][:], in0=n[i][:], in1=step[i][:], op=ALU.add)
+            return res
+
+        out_view = out.rearrange("(t b) n -> b t n", b=P)
+
+        def store(rnd, res):
+            for i in range(ROUND_TILES):
+                m = ROUND_TILES * rnd + i
+                bank = psum.tile([P, BATCH_TILES, P], F32, name="res_T", tag="bank")
+                for bt in range(BATCH_TILES):
+                    nc.tensor.transpose(bank[:, bt, :], res[i][:, P * bt : P * (bt + 1)], ident_f32[:])
+                final = work.tile([P, BATCH_TILES, P], F32, name="final")
+                nc.scalar.copy(out=final[:], in_=bank[:])
+                nc.sync.dma_start(out=out_view[:, :, P * m : P * (m + 1)], in_=final[:])
+
+        results = {}
+        for rnd in range(ROUNDS):
+            results[rnd] = gates(rnd, multiply(rnd))
+            if rnd > 0:
+                store(rnd - 1, results[rnd - 1])
+        store(ROUNDS - 1, results[ROUNDS - 1])

@@ -20,19 +20,10 @@ K_PASS = 4 * P
 PASSES = K // K_PASS
 BATCH_TILES = BATCH // P
 FEATURE_TILES = FEATURES // P
-ROUND_TILES = 2
-ROUNDS = FEATURE_TILES // ROUND_TILES
-ROUND_COLS = ROUND_TILES * P
+HALF = 512
+HALVES = FEATURES // HALF
 
 FLOPS = 2 * BATCH * K * FEATURES * 6
-
-PRODUCTS = (
-    ("r", (("x", "Wir"), ("h", "Whr"))),
-    ("hn", (("h", "Whn"),)),
-    ("in", (("x", "Win"),)),
-    ("z", (("x", "Wiz"), ("h", "Whz"))),
-)
-WEIGHT_ORDER = ("Wir", "Whr", "Whn", "Win", "Wiz", "Whz")
 
 
 def tile_gru_kernel(
@@ -68,64 +59,89 @@ def tile_gru_kernel(
     with ExitStack() as stack:
         stack.enter_context(tc.manual_schedule())
         keep = stack.enter_context(tc.tile_pool(name="keep", bufs=1))
-        work = stack.enter_context(tc.tile_pool(name="work", bufs=ROUND_TILES + 1))
-        late = stack.enter_context(tc.tile_pool(name="late", bufs=2 * ROUND_TILES + 1))
+        work = stack.enter_context(tc.tile_pool(name="work", bufs=3))
         psum = stack.enter_context(tc.psum_pool(name="psum", bufs=8))
-
-        planes = {}
-        plane_offset = {}
-        for index, name in enumerate(WEIGHT_ORDER):
-            if index % 2 == 0:
-                shared = keep.tile([P, FEATURES], U8, name="planes_%d" % (index // 2), align_bytes=64)
-                nc.vector.memset(shared[:].bitcast(I32), 0)
-            planes[name] = shared
-            plane_offset[name] = 8 * (index % 2)
-        bias_rows = keep.tile([P, P], BF16, name="bias_rows")
-        nc.vector.memset(bias_rows[:], 0.0)
-        zero_col = keep.tile([P, 1], F32, name="zero_col")
-        nc.vector.memset(zero_col[:], 0.0)
 
         ident_f32 = keep.tile([P, P], F32, name="ident_f32")
         make_identity(nc, ident_f32[:])
-        ident_bf16 = keep.tile([P, P], BF16, name="ident_bf16")
-        make_identity(nc, ident_bf16[:])
 
+        zero_col = keep.tile([P, 1], F32, name="zero_col")
+        nc.vector.memset(zero_col[:], 0.0)
         warm_col = keep.tile([P, 1], F32, name="warm_col")
         nc.scalar.activation(out=warm_col[:], in_=zero_col[:], func=ACT.Sigmoid)
 
-        for index, name in enumerate(WEIGHT_ORDER):
-            nc.gpsimd.dma_start(
-                out=bias_rows[FEATURE_TILES * index : FEATURE_TILES * (index + 1), :],
-                in_=dram_bias[name].rearrange("(m j) -> m j", j=P),
-            )
+        bias_z_rows = keep.tile([P, FEATURES], BF16, name="bias_z_rows")
+        nc.vector.memset(bias_z_rows[:].bitcast(I32), 0)
+        bias_n_rows = keep.tile([P, FEATURES], BF16, name="bias_n_rows")
+        nc.vector.memset(bias_n_rows[:].bitcast(I32), 0)
+        planes = {}
+
+        def clear_planes(name):
+            planes[name] = keep.tile([P, FEATURES], U8, name="planes_" + name, align_bytes=64)
+            nc.vector.memset(planes[name][:].bitcast(I32), 0)
+
+        clear_planes("Wiz")
+        clear_planes("Whz")
+        pick = keep.tile([P, P + 4], BF16, name="pick")
+        nc.vector.memset(pick[:], 0.0)
+        nc.vector.memset(pick[0:2, 0:P], 1.0)
+        nc.vector.memset(pick[32:34, P : P + 1], 1.0)
+        nc.vector.memset(pick[64:65, P + 1 : P + 2], 1.0)
+        nc.vector.memset(pick[96:97, P + 2 : P + 3], 1.0)
+        for name in ("Wir", "Whr", "Whn", "Win"):
+            clear_planes(name)
+
+        def load_bias(tile, row, name):
+            nc.gpsimd.dma_start(out=tile[row : row + 1, :], in_=dram_bias[name].rearrange("(o n) -> o n", o=1))
 
         rows = {}
         for act in ("x", "h"):
-            for bt in range(BATCH_TILES):
-                rows[act, bt] = keep.tile([P, K], BF16, name="rows_%s_%d" % (act, bt))
-                nc.sync.dma_start(out=rows[act, bt][:], in_=dram_rows[act][P * bt : P * (bt + 1), :])
+            rows[act] = keep.tile([P, BATCH_TILES, K], BF16, name="rows_" + act)
+
+        def load_rows(act, first, last):
+            source = dram_rows[act].rearrange("(t b) k -> b t k", b=P)
+            nc.sync.dma_start(out=rows[act][:, first:last, :], in_=source[:, first:last, :])
 
         words = {}
 
-        def load_words(name, rnd):
-            words[name, rnd] = keep.tile([P, PASSES, ROUND_COLS], I32, name="words_%s_%d" % (name, rnd), align_bytes=64)
+        def load_words(name, half):
+            words[name, half] = keep.tile([P, PASSES, HALF], I32, name="words_%s_%d" % (name, half), align_bytes=64)
             source = dram_words[name].rearrange("g p n t -> p g (n t)")
             nc.sync.dma_start(
-                out=words[name, rnd][:],
-                in_=source[:, :, 4 * ROUND_COLS * rnd : 4 * ROUND_COLS * (rnd + 1)].bitcast(I32),
+                out=words[name, half][:],
+                in_=source[:, :, 4 * HALF * half : 4 * HALF * (half + 1)].bitcast(I32),
             )
 
-        for name in WEIGHT_ORDER:
+        def load_scales(name):
             for quadrant in range(4):
-                first = 32 * quadrant + plane_offset[name]
                 nc.sync.dma_start(
-                    out=planes[name][first : first + 4 * PASSES, :].bitcast(I32),
+                    out=planes[name][32 * quadrant : 32 * quadrant + 4 * PASSES, :].bitcast(I32),
                     in_=dram_scales[name][:, 4 * quadrant : 4 * quadrant + 4, :].bitcast(I32),
                 )
+
+        load_bias(bias_z_rows, 0, "Wiz")
+        load_bias(bias_z_rows, 1, "Whz")
+        load_bias(bias_n_rows, 32, "Wir")
+        load_bias(bias_n_rows, 33, "Whr")
+        load_bias(bias_n_rows, 64, "Whn")
+        load_bias(bias_n_rows, 96, "Win")
+
+        load_rows("x", 0, 1)
+        load_rows("x", 1, 2)
+        load_rows("x", 2, 4)
+        load_rows("h", 0, 2)
+        load_rows("h", 2, 4)
+        load_scales("Wiz")
+        load_words("Wiz", 0)
+        load_words("Whz", 0)
+        load_scales("Whz")
+        load_words("Wiz", 1)
+        load_words("Whz", 1)
+        for name in ("Wir", "Whr", "Whn", "Win"):
+            load_scales(name)
             load_words(name, 0)
-        for rnd in range(1, ROUNDS):
-            for name in WEIGHT_ORDER:
-                load_words(name, rnd)
+        for name in ("Wir", "Whr", "Whn", "Win"):
+            load_words(name, 1)
 
         grouped = {}
         codes = {}
@@ -135,20 +151,18 @@ def tile_gru_kernel(
             codes[act] = keep.tile([P, PASSES, BATCH], U32, name="codes_" + act, align_bytes=64)
             act_planes[act] = keep.tile([P, PASSES, BATCH], U8, name="act_planes_" + act, align_bytes=64)
 
-        def copy_out(index, out_ap, in_ap):
-            if index % 2 == 0:
-                nc.vector.tensor_copy(out=out_ap, in_=in_ap)
-            else:
-                nc.scalar.copy(out=out_ap, in_=in_ap)
-
         def transpose_pairs(index, act, bt):
-            pairs = rows[act, bt][:].bitcast(F32)
+            pairs = rows[act][:, bt, :].bitcast(F32)
             bank = psum.tile([P, PASSES, 2, P], F32, name="pairs_T", tag="bank")
             for g in range(PASSES):
                 for u in range(2):
                     nc.tensor.transpose(bank[:, g, u, :], pairs[:, 256 * g + u : 256 * (g + 1) : 2], ident_f32[:])
-            target = grouped[act][:].bitcast(F32).rearrange("p g (b u) -> p g b u", u=2)
-            copy_out(index, target[:, :, P * bt : P * (bt + 1), :], bank[:].rearrange("p g u b -> p g b u"))
+            target = grouped[act][:].bitcast(F32).rearrange("p g (b u) -> p g b u", u=2)[:, :, P * bt : P * (bt + 1), :]
+            source = bank[:].rearrange("p g u b -> p g b u")
+            if index % 2 == 0:
+                nc.vector.tensor_copy(out=target, in_=source)
+            else:
+                nc.scalar.copy(out=target, in_=source)
 
         def quantise(act, bt):
             for g in range(PASSES):
@@ -165,97 +179,113 @@ def tile_gru_kernel(
                 quantise(*row_tiles[index - 1])
         quantise(*row_tiles[-1])
 
-        hidden_T = keep.tile([P, FEATURE_TILES, BATCH], BF16, name="hidden_T")
-        for half in range(FEATURE_TILES // 2):
-            bank = psum.tile([P, 2, BATCH_TILES, P], BF16, name="hidden_T_bank", tag="bank")
-            for i in range(2):
-                m = 2 * half + i
+        bias_z = keep.tile([P, FEATURES], F32, name="bias_z")
+        for half in range(HALVES):
+            cols = slice(HALF * half, HALF * (half + 1))
+            bank = psum.tile([P, HALF], F32, name="bias_z_bank", tag="bank")
+            nc.tensor.matmul(bank[:], lhsT=pick[:, 0:P], rhs=bias_z_rows[:, cols], start=True, stop=True)
+            nc.scalar.copy(out=bias_z[:, cols], in_=bank[:])
+
+        z = keep.tile([P, BATCH_TILES, FEATURES], F32, name="z")
+        zh = keep.tile([P, BATCH_TILES, FEATURES], F32, name="zh")
+
+        def z_products(half):
+            cols = slice(HALF * half, HALF * (half + 1))
+            banks = []
+            for bt in range(BATCH_TILES):
+                bank = psum.tile([P, HALF], F32, name="bank_z", tag="bank")
+                banks.append(bank)
+            for act, name in (("x", "Wiz"), ("h", "Whz")):
                 for bt in range(BATCH_TILES):
-                    nc.tensor.transpose(bank[:, i, bt, :], rows["h", bt][:, P * m : P * (m + 1)], ident_bf16[:])
-            copy_out(
-                half,
-                hidden_T[:, 2 * half : 2 * half + 2, :].rearrange("p m b -> p (m b)"),
-                bank[:].rearrange("p i t b -> p (i t b)"),
-            )
-
-        bias_bank = psum.tile([P, P], BF16, name="bias_bank", tag="bank")
-        nc.tensor.transpose(bias_bank[:], bias_rows[:], ident_bf16[:])
-        bias_cols = keep.tile([P, len(WEIGHT_ORDER) * FEATURE_TILES], F32, name="bias_cols")
-        nc.vector.tensor_copy(out=bias_cols[:], in_=bias_bank[:, 0 : len(WEIGHT_ORDER) * FEATURE_TILES])
-        bias = {}
-        for index, name in enumerate(WEIGHT_ORDER):
-            bias[name] = bias_cols[:, FEATURE_TILES * index : FEATURE_TILES * (index + 1)]
-        bias_r = keep.tile([P, FEATURE_TILES], F32, name="bias_r")
-        nc.vector.tensor_tensor(out=bias_r[:], in0=bias["Wir"], in1=bias["Whr"], op=ALU.add)
-        bias_z = keep.tile([P, FEATURE_TILES], F32, name="bias_z")
-        nc.vector.tensor_tensor(out=bias_z[:], in0=bias["Wiz"], in1=bias["Whz"], op=ALU.add)
-
-        def multiply(rnd):
-            banks = {}
-            for product, pairs in PRODUCTS:
-                for i in range(ROUND_TILES):
-                    m = ROUND_TILES * rnd + i
-                    bank = psum.tile([P, BATCH], F32, name="bank_" + product, tag="bank")
-                    banks[product, i] = bank
-                    steps = [(act, name, g) for act, name in pairs for g in range(PASSES)]
-                    for step, (act, name, g) in enumerate(steps):
+                    batch_rows = slice(P * bt, P * (bt + 1))
+                    for g in range(PASSES):
                         nc.tensor.matmul_mx(
-                            out=bank[:],
-                            lhsT=words[name, rnd][:, g, P * i : P * (i + 1)].bitcast(FP8X4),
-                            lhsT_scale=planes[name][plane_offset[name] + 4 * g : P, P * m : P * (m + 1)],
-                            rhs=codes[act][:, g, :].bitcast(FP8X4),
-                            rhs_scale=act_planes[act][:, g, :],
-                            start=(step == 0),
-                            stop=(step == len(steps) - 1),
+                            out=banks[bt][:],
+                            lhsT=codes[act][:, g, batch_rows].bitcast(FP8X4),
+                            lhsT_scale=act_planes[act][:, g, batch_rows],
+                            rhs=words[name, half][:, g, :].bitcast(FP8X4),
+                            rhs_scale=planes[name][4 * g : P, cols],
+                            start=(act == "x" and g == 0),
+                            stop=(act == "h" and g == PASSES - 1),
                         )
-            return banks
+            for bt in range(BATCH_TILES):
+                z_in = work.tile([P, HALF], F32, name="z_in")
+                nc.vector.tensor_tensor(out=z_in[:], in0=banks[bt][:], in1=bias_z[:, cols], op=ALU.add)
+                nc.scalar.activation(out=z[:, bt, cols], in_=z_in[:], func=ACT.Sigmoid)
+                nc.gpsimd.tensor_tensor(out=zh[:, bt, cols], in0=z[:, bt, cols], in1=rows["h"][:, bt, cols], op=ALU.mult)
 
-        def gates(rnd, banks):
-            tiles = range(ROUND_TILES)
-            cols = [slice(ROUND_TILES * rnd + i, ROUND_TILES * rnd + i + 1) for i in tiles]
-            r, rh, pre, n, z, diff, step, res = {}, {}, {}, {}, {}, {}, {}, {}
-            for i in tiles:
-                r[i] = work.tile([P, BATCH], F32, name="r")
-                nc.scalar.activation(out=r[i][:], in_=banks["r", i][:], func=ACT.Sigmoid, bias=bias_r[:, cols[i]])
-            for i in tiles:
-                rh[i] = work.tile([P, BATCH], F32, name="rh")
-                nc.vector.scalar_tensor_tensor(
-                    out=rh[i][:], in0=banks["hn", i][:], scalar=bias["Whn"][:, cols[i]], in1=r[i][:], op0=ALU.add, op1=ALU.mult
+        for half in range(HALVES):
+            z_products(half)
+
+        bias_bank = psum.tile([P, FEATURE_TILES, 4], F32, name="bias_bank", tag="bank")
+        for m in range(FEATURE_TILES):
+            nc.tensor.matmul(bias_bank[:, m, :], lhsT=bias_n_rows[:, P * m : P * (m + 1)], rhs=pick[:, P : P + 4], start=True, stop=True)
+        bias_cols = keep.tile([P, FEATURE_TILES, 4], F32, name="bias_cols")
+        nc.vector.tensor_copy(out=bias_cols[:], in_=bias_bank[:])
+
+        def product(label, pairs, m):
+            half, tile_in_half = divmod(m, HALF // P)
+            bank = psum.tile([P, BATCH], F32, name="bank_" + label, tag="bank")
+            steps = [(act, name, g) for act, name in pairs for g in range(PASSES)]
+            for step, (act, name, g) in enumerate(steps):
+                nc.tensor.matmul_mx(
+                    out=bank[:],
+                    lhsT=words[name, half][:, g, P * tile_in_half : P * (tile_in_half + 1)].bitcast(FP8X4),
+                    lhsT_scale=planes[name][4 * g : P, P * m : P * (m + 1)],
+                    rhs=codes[act][:, g, :].bitcast(FP8X4),
+                    rhs_scale=act_planes[act][:, g, :],
+                    start=(step == 0),
+                    stop=(step == len(steps) - 1),
                 )
-            for i in tiles:
-                pre[i] = work.tile([P, BATCH], F32, name="pre")
-                nc.vector.tensor_tensor(out=pre[i][:], in0=banks["in", i][:], in1=rh[i][:], op=ALU.add)
-            for i in tiles:
-                n[i] = work.tile([P, BATCH], F32, name="n")
-                nc.scalar.activation(out=n[i][:], in_=pre[i][:], func=ACT.Tanh, bias=bias["Win"][:, cols[i]])
-            for i in tiles:
-                diff[i] = work.tile([P, BATCH], F32, name="diff")
-                nc.vector.tensor_tensor(out=diff[i][:], in0=hidden_T[:, ROUND_TILES * rnd + i, :], in1=n[i][:], op=ALU.subtract)
-            for i in tiles:
-                z[i] = work.tile([P, BATCH], F32, name="z")
-                nc.scalar.activation(out=z[i][:], in_=banks["z", i][:], func=ACT.Sigmoid, bias=bias_z[:, cols[i]])
-            for i in tiles:
-                step[i] = work.tile([P, BATCH], F32, name="step")
-                nc.vector.tensor_tensor(out=step[i][:], in0=z[i][:], in1=diff[i][:], op=ALU.mult)
-                res[i] = late.tile([P, BATCH], F32, name="res")
-                nc.vector.tensor_tensor(out=res[i][:], in0=n[i][:], in1=step[i][:], op=ALU.add)
-            return res
+            return bank
+
+        r = {}
+        n = {}
+
+        def make_r(m):
+            bank = product("r", (("x", "Wir"), ("h", "Whr")), m)
+            r[m] = work.tile([P, BATCH], F32, name="r")
+            nc.scalar.activation(out=r[m][:], in_=bank[:], func=ACT.Sigmoid, bias=bias_cols[:, m, 0:1])
+
+        def make_n(m):
+            bank_hn = product("hn", (("h", "Whn"),), m)
+            bank_in = product("in", (("x", "Win"),), m)
+            rh = work.tile([P, BATCH], F32, name="rh")
+            nc.vector.scalar_tensor_tensor(
+                out=rh[:], in0=bank_hn[:], scalar=bias_cols[:, m, 1:2], in1=r[m][:], op0=ALU.add, op1=ALU.mult
+            )
+            n_in = work.tile([P, BATCH], F32, name="n_in")
+            nc.vector.tensor_tensor(out=n_in[:], in0=bank_in[:], in1=rh[:], op=ALU.add)
+            n[m] = work.tile([P, BATCH], F32, name="n")
+            nc.scalar.activation(out=n[m][:], in_=n_in[:], func=ACT.Tanh, bias=bias_cols[:, m, 2:3])
 
         out_view = out.rearrange("(t b) n -> b t n", b=P)
 
-        def store(rnd, res):
-            for i in range(ROUND_TILES):
-                m = ROUND_TILES * rnd + i
-                bank = psum.tile([P, BATCH_TILES, P], F32, name="res_T", tag="bank")
-                for bt in range(BATCH_TILES):
-                    nc.tensor.transpose(bank[:, bt, :], res[i][:, P * bt : P * (bt + 1)], ident_f32[:])
-                final = work.tile([P, BATCH_TILES, P], F32, name="final")
-                nc.scalar.copy(out=final[:], in_=bank[:])
-                nc.sync.dma_start(out=out_view[:, :, P * m : P * (m + 1)], in_=final[:])
+        def transpose_n(m):
+            bank = psum.tile([P, BATCH_TILES, P], F32, name="n_T", tag="bank")
+            for bt in range(BATCH_TILES):
+                nc.tensor.transpose(bank[:, bt, :], n[m][:, P * bt : P * (bt + 1)], ident_f32[:])
+            return bank
 
-        results = {}
-        for rnd in range(ROUNDS):
-            results[rnd] = gates(rnd, multiply(rnd))
-            if rnd > 0:
-                store(rnd - 1, results[rnd - 1])
-        store(ROUNDS - 1, results[ROUNDS - 1])
+        def blend(m, bank, adder):
+            cols = slice(P * m, P * (m + 1))
+            part = work.tile([P, BATCH_TILES, P], F32, name="part")
+            nc.vector.scalar_tensor_tensor(out=part[:], in0=z[:, :, cols], scalar=1.0, in1=bank[:], op0=ALU.subtract, op1=ALU.mult)
+            res = work.tile([P, BATCH_TILES, P], F32, name="res")
+            adder.tensor_tensor(out=res[:], in0=zh[:, :, cols], in1=part[:], op=ALU.subtract)
+            nc.sync.dma_start(out=out_view[:, :, cols], in_=res[:])
+
+        last = FEATURE_TILES - 1
+        make_r(0)
+        for m in range(last):
+            if m + 1 < last:
+                make_r(m + 1)
+            make_n(m)
+            if m > 0 and m % 2 == 0:
+                banks = [transpose_n(m - 2), transpose_n(m - 1)]
+                blend(m - 2, banks[0], nc.gpsimd)
+                blend(m - 1, banks[1], nc.gpsimd)
+        make_r(last)
+        make_n(last)
+        for m in (last - 1, last):
+            blend(m, transpose_n(m), nc.vector)

@@ -59,7 +59,7 @@ def tile_gru_kernel(
     with ExitStack() as stack:
         stack.enter_context(tc.manual_schedule())
         keep = stack.enter_context(tc.tile_pool(name="keep", bufs=1))
-        work = stack.enter_context(tc.tile_pool(name="work", bufs=3))
+        work = stack.enter_context(tc.tile_pool(name="work", bufs=4))
         psum = stack.enter_context(tc.psum_pool(name="psum", bufs=8))
 
         ident_f32 = keep.tile([P, P], F32, name="ident_f32")
@@ -72,7 +72,7 @@ def tile_gru_kernel(
 
         bias_z_rows = keep.tile([P, FEATURES], BF16, name="bias_z_rows")
         nc.vector.memset(bias_z_rows[:].bitcast(I32), 0)
-        bias_n_rows = keep.tile([P, FEATURES], BF16, name="bias_n_rows")
+        bias_n_rows = keep.tile([P, P], BF16, name="bias_n_rows")
         nc.vector.memset(bias_n_rows[:].bitcast(I32), 0)
         planes = {}
 
@@ -82,17 +82,14 @@ def tile_gru_kernel(
 
         clear_planes("Wiz")
         clear_planes("Whz")
-        pick = keep.tile([P, P + 4], BF16, name="pick")
-        nc.vector.memset(pick[:], 0.0)
-        nc.vector.memset(pick[0:2, 0:P], 1.0)
-        nc.vector.memset(pick[32:34, P : P + 1], 1.0)
-        nc.vector.memset(pick[64:65, P + 1 : P + 2], 1.0)
-        nc.vector.memset(pick[96:97, P + 2 : P + 3], 1.0)
+        add_rows = keep.tile([P, P], BF16, name="add_rows")
+        nc.vector.memset(add_rows[:], 0.0)
+        nc.vector.memset(add_rows[0:2, :], 1.0)
+        ident_bf16 = keep.tile([P, P], BF16, name="ident_bf16")
+        nc.vector.tensor_copy(out=ident_bf16[:], in_=ident_f32[:])
         for name in ("Wir", "Whr", "Whn", "Win"):
             clear_planes(name)
 
-        def load_bias(tile, row, name):
-            nc.gpsimd.dma_start(out=tile[row : row + 1, :], in_=dram_bias[name].rearrange("(o n) -> o n", o=1))
 
         rows = {}
         for act in ("x", "h"):
@@ -119,12 +116,13 @@ def tile_gru_kernel(
                     in_=dram_scales[name][:, 4 * quadrant : 4 * quadrant + 4, :].bitcast(I32),
                 )
 
-        load_bias(bias_z_rows, 0, "Wiz")
-        load_bias(bias_z_rows, 1, "Whz")
-        load_bias(bias_n_rows, 32, "Wir")
-        load_bias(bias_n_rows, 33, "Whr")
-        load_bias(bias_n_rows, 64, "Whn")
-        load_bias(bias_n_rows, 96, "Win")
+        for row, name in enumerate(("Wiz", "Whz")):
+            nc.gpsimd.dma_start(out=bias_z_rows[row : row + 1, :], in_=dram_bias[name].rearrange("(o n) -> o n", o=1))
+        for index, name in enumerate(("Wir", "Whr", "Whn", "Win")):
+            nc.gpsimd.dma_start(
+                out=bias_n_rows[FEATURE_TILES * index : FEATURE_TILES * (index + 1), :],
+                in_=dram_bias[name].rearrange("(m j) -> m j", j=P),
+            )
 
         load_rows("x", 0, 1)
         load_rows("x", 1, 2)
@@ -136,10 +134,15 @@ def tile_gru_kernel(
         load_words("Whz", 0)
         load_scales("Whz")
         load_words("Wiz", 1)
+        load_scales("Wir")
         load_words("Whz", 1)
-        for name in ("Wir", "Whr", "Whn", "Win"):
-            load_scales(name)
-            load_words(name, 0)
+        load_scales("Whr")
+        load_words("Wir", 0)
+        load_scales("Whn")
+        load_words("Whr", 0)
+        load_scales("Win")
+        load_words("Whn", 0)
+        load_words("Win", 0)
         for name in ("Wir", "Whr", "Whn", "Win"):
             load_words(name, 1)
 
@@ -183,7 +186,7 @@ def tile_gru_kernel(
         for half in range(HALVES):
             cols = slice(HALF * half, HALF * (half + 1))
             bank = psum.tile([P, HALF], F32, name="bias_z_bank", tag="bank")
-            nc.tensor.matmul(bank[:], lhsT=pick[:, 0:P], rhs=bias_z_rows[:, cols], start=True, stop=True)
+            nc.tensor.matmul(bank[:], lhsT=add_rows[:], rhs=bias_z_rows[:, cols], start=True, stop=True)
             nc.scalar.copy(out=bias_z[:, cols], in_=bank[:])
 
         z = keep.tile([P, BATCH_TILES, FEATURES], F32, name="z")
@@ -214,78 +217,92 @@ def tile_gru_kernel(
                 nc.scalar.activation(out=z[:, bt, cols], in_=z_in[:], func=ACT.Sigmoid)
                 nc.gpsimd.tensor_tensor(out=zh[:, bt, cols], in0=z[:, bt, cols], in1=rows["h"][:, bt, cols], op=ALU.mult)
 
-        for half in range(HALVES):
-            z_products(half)
+        z_products(0)
 
-        bias_bank = psum.tile([P, FEATURE_TILES, 4], F32, name="bias_bank", tag="bank")
-        for m in range(FEATURE_TILES):
-            nc.tensor.matmul(bias_bank[:, m, :], lhsT=bias_n_rows[:, P * m : P * (m + 1)], rhs=pick[:, P : P + 4], start=True, stop=True)
-        bias_cols = keep.tile([P, FEATURE_TILES, 4], F32, name="bias_cols")
-        nc.vector.tensor_copy(out=bias_cols[:], in_=bias_bank[:])
+        bias_bank = psum.tile([P, P], BF16, name="bias_bank", tag="bank")
+        nc.tensor.transpose(bias_bank[:], bias_n_rows[:], ident_bf16[:])
+        bias_cols = keep.tile([P, 4 * FEATURE_TILES], F32, name="bias_cols")
+        nc.vector.tensor_copy(out=bias_cols[:], in_=bias_bank[:, 0 : 4 * FEATURE_TILES])
+        bias_r = keep.tile([P, FEATURE_TILES], F32, name="bias_r")
+        nc.vector.tensor_tensor(
+            out=bias_r[:], in0=bias_cols[:, 0:FEATURE_TILES], in1=bias_cols[:, FEATURE_TILES : 2 * FEATURE_TILES], op=ALU.add
+        )
+        bias_hn = bias_cols[:, 2 * FEATURE_TILES : 3 * FEATURE_TILES]
+        bias_in = bias_cols[:, 3 * FEATURE_TILES : 4 * FEATURE_TILES]
 
-        def product(label, pairs, m):
+        z_products(1)
+
+        def product(label, pairs, m, batch):
             half, tile_in_half = divmod(m, HALF // P)
-            bank = psum.tile([P, BATCH], F32, name="bank_" + label, tag="bank")
+            bank = psum.tile([P, batch.stop - batch.start], F32, name="bank_" + label, tag="bank")
             steps = [(act, name, g) for act, name in pairs for g in range(PASSES)]
             for step, (act, name, g) in enumerate(steps):
                 nc.tensor.matmul_mx(
                     out=bank[:],
                     lhsT=words[name, half][:, g, P * tile_in_half : P * (tile_in_half + 1)].bitcast(FP8X4),
                     lhsT_scale=planes[name][4 * g : P, P * m : P * (m + 1)],
-                    rhs=codes[act][:, g, :].bitcast(FP8X4),
-                    rhs_scale=act_planes[act][:, g, :],
+                    rhs=codes[act][:, g, batch].bitcast(FP8X4),
+                    rhs_scale=act_planes[act][:, g, batch],
                     start=(step == 0),
                     stop=(step == len(steps) - 1),
                 )
             return bank
 
         r = {}
+        rh = {}
         n = {}
+        whole = slice(0, BATCH)
 
         def make_r(m):
-            bank = product("r", (("x", "Wir"), ("h", "Whr")), m)
+            bank = product("r", (("x", "Wir"), ("h", "Whr")), m, whole)
             r[m] = work.tile([P, BATCH], F32, name="r")
-            nc.scalar.activation(out=r[m][:], in_=bank[:], func=ACT.Sigmoid, bias=bias_cols[:, m, 0:1])
-
-        def make_n(m):
-            bank_hn = product("hn", (("h", "Whn"),), m)
-            bank_in = product("in", (("x", "Win"),), m)
-            rh = work.tile([P, BATCH], F32, name="rh")
-            nc.vector.scalar_tensor_tensor(
-                out=rh[:], in0=bank_hn[:], scalar=bias_cols[:, m, 1:2], in1=r[m][:], op0=ALU.add, op1=ALU.mult
-            )
-            n_in = work.tile([P, BATCH], F32, name="n_in")
-            nc.vector.tensor_tensor(out=n_in[:], in0=bank_in[:], in1=rh[:], op=ALU.add)
+            nc.scalar.activation(out=r[m][:], in_=bank[:], func=ACT.Sigmoid, bias=bias_r[:, m : m + 1])
+            rh[m] = work.tile([P, BATCH], F32, name="rh")
             n[m] = work.tile([P, BATCH], F32, name="n")
-            nc.scalar.activation(out=n[m][:], in_=n_in[:], func=ACT.Tanh, bias=bias_cols[:, m, 2:3])
+
+        def make_rh(m, batch):
+            bank = product("hn", (("h", "Whn"),), m, batch)
+            nc.vector.scalar_tensor_tensor(
+                out=rh[m][:, batch], in0=bank[:], scalar=bias_hn[:, m : m + 1], in1=r[m][:, batch], op0=ALU.add, op1=ALU.mult
+            )
+
+        def make_n(m, batch):
+            bank = product("in", (("x", "Win"),), m, batch)
+            n_in = work.tile([P, batch.stop - batch.start], F32, name="n_in")
+            nc.vector.tensor_tensor(out=n_in[:], in0=bank[:], in1=rh[m][:, batch], op=ALU.add)
+            nc.scalar.activation(out=n[m][:, batch], in_=n_in[:], func=ACT.Tanh, bias=bias_in[:, m : m + 1])
 
         out_view = out.rearrange("(t b) n -> b t n", b=P)
 
-        def transpose_n(m):
-            bank = psum.tile([P, BATCH_TILES, P], F32, name="n_T", tag="bank")
-            for bt in range(BATCH_TILES):
-                nc.tensor.transpose(bank[:, bt, :], n[m][:, P * bt : P * (bt + 1)], ident_f32[:])
-            return bank
-
-        def blend(m, bank, adder):
+        def blend(m, tiles, adder):
             cols = slice(P * m, P * (m + 1))
-            part = work.tile([P, BATCH_TILES, P], F32, name="part")
-            nc.vector.scalar_tensor_tensor(out=part[:], in0=z[:, :, cols], scalar=1.0, in1=bank[:], op0=ALU.subtract, op1=ALU.mult)
-            res = work.tile([P, BATCH_TILES, P], F32, name="res")
-            adder.tensor_tensor(out=res[:], in0=zh[:, :, cols], in1=part[:], op=ALU.subtract)
-            nc.sync.dma_start(out=out_view[:, :, cols], in_=res[:])
+            span = slice(tiles.start, tiles.stop)
+            bank = psum.tile([P, len(tiles), P], F32, name="n_T", tag="bank")
+            for index, bt in enumerate(tiles):
+                nc.tensor.transpose(bank[:, index, :], n[m][:, P * bt : P * (bt + 1)], ident_f32[:])
+            part = work.tile([P, len(tiles), P], F32, name="part")
+            nc.vector.scalar_tensor_tensor(out=part[:], in0=z[:, span, cols], scalar=1.0, in1=bank[:], op0=ALU.subtract, op1=ALU.mult)
+            res = work.tile([P, len(tiles), P], F32, name="res")
+            adder.tensor_tensor(out=res[:], in0=zh[:, span, cols], in1=part[:], op=ALU.subtract)
+            nc.sync.dma_start(out=out_view[:, span, cols], in_=res[:])
 
+        all_tiles = range(BATCH_TILES)
         last = FEATURE_TILES - 1
+        blended_in_turn = {3: (0, 1), 5: (2, 3), 6: (4,)}
         make_r(0)
-        for m in range(last):
-            if m + 1 < last:
-                make_r(m + 1)
-            make_n(m)
-            if m > 0 and m % 2 == 0:
-                banks = [transpose_n(m - 2), transpose_n(m - 1)]
-                blend(m - 2, banks[0], nc.gpsimd)
-                blend(m - 1, banks[1], nc.gpsimd)
-        make_r(last)
-        make_n(last)
-        for m in (last - 1, last):
-            blend(m, transpose_n(m), nc.vector)
+        for turn in range(last):
+            make_r(turn + 1)
+            make_rh(turn, whole)
+            if turn > 0:
+                make_n(turn - 1, whole)
+            for m in blended_in_turn.get(turn, ()):
+                blend(m, all_tiles, nc.gpsimd)
+        halves = [range(0, BATCH_TILES // 2), range(BATCH_TILES // 2, BATCH_TILES)]
+        make_rh(last, whole)
+        make_n(last - 1, whole)
+        blend(last - 2, all_tiles, nc.gpsimd)
+        for tiles in halves:
+            make_n(last, slice(P * tiles.start, P * tiles.stop))
+        blend(last - 1, all_tiles, nc.gpsimd)
+        for tiles in halves:
+            blend(last, tiles, nc.vector)

@@ -127,10 +127,10 @@ def tile_gru_kernel(
         load_rows("x", 0, 1)
         load_rows("x", 1, 2)
         load_rows("x", 2, 4)
-        load_rows("h", 0, 2)
-        load_rows("h", 2, 4)
         load_scales("Wiz")
         load_words("Wiz", 0)
+        load_rows("h", 0, 2)
+        load_rows("h", 2, 4)
         load_words("Whz", 0)
         load_scales("Whz")
         load_words("Wiz", 1)
@@ -175,49 +175,57 @@ def tile_gru_kernel(
                     in_=grouped[act][:, g, 4 * P * bt : 4 * P * (bt + 1)],
                 )
 
-        row_tiles = [(act, bt) for act in ("x", "h") for bt in range(BATCH_TILES)]
-        for index, (act, bt) in enumerate(row_tiles):
-            transpose_pairs(index, act, bt)
-            if index > 0:
-                quantise(*row_tiles[index - 1])
-        quantise(*row_tiles[-1])
-
         bias_z = keep.tile([P, FEATURES], F32, name="bias_z")
-        for half in range(HALVES):
+        z = keep.tile([P, BATCH_TILES, FEATURES], F32, name="z")
+        zh = keep.tile([P, BATCH_TILES, FEATURES], F32, name="zh")
+        z_banks = {}
+
+        def spread_bias_z(half):
             cols = slice(HALF * half, HALF * (half + 1))
             bank = psum.tile([P, HALF], F32, name="bias_z_bank", tag="bank")
             nc.tensor.matmul(bank[:], lhsT=add_rows[:], rhs=bias_z_rows[:, cols], start=True, stop=True)
             nc.scalar.copy(out=bias_z[:, cols], in_=bank[:])
 
-        z = keep.tile([P, BATCH_TILES, FEATURES], F32, name="z")
-        zh = keep.tile([P, BATCH_TILES, FEATURES], F32, name="zh")
+        def z_passes(act, name, half, bt):
+            if act == "x":
+                z_banks[half, bt] = psum.tile([P, HALF], F32, name="bank_z", tag="bank")
+            batch_rows = slice(P * bt, P * (bt + 1))
+            for g in range(PASSES):
+                nc.tensor.matmul_mx(
+                    out=z_banks[half, bt][:],
+                    lhsT=codes[act][:, g, batch_rows].bitcast(FP8X4),
+                    lhsT_scale=act_planes[act][:, g, batch_rows],
+                    rhs=words[name, half][:, g, :].bitcast(FP8X4),
+                    rhs_scale=planes[name][4 * g : P, HALF * half : HALF * (half + 1)],
+                    start=(act == "x" and g == 0),
+                    stop=(act == "h" and g == PASSES - 1),
+                )
 
-        def z_products(half):
+        def finish_z(half, bt):
             cols = slice(HALF * half, HALF * (half + 1))
-            banks = []
-            for bt in range(BATCH_TILES):
-                bank = psum.tile([P, HALF], F32, name="bank_z", tag="bank")
-                banks.append(bank)
-            for act, name in (("x", "Wiz"), ("h", "Whz")):
-                for bt in range(BATCH_TILES):
-                    batch_rows = slice(P * bt, P * (bt + 1))
-                    for g in range(PASSES):
-                        nc.tensor.matmul_mx(
-                            out=banks[bt][:],
-                            lhsT=codes[act][:, g, batch_rows].bitcast(FP8X4),
-                            lhsT_scale=act_planes[act][:, g, batch_rows],
-                            rhs=words[name, half][:, g, :].bitcast(FP8X4),
-                            rhs_scale=planes[name][4 * g : P, cols],
-                            start=(act == "x" and g == 0),
-                            stop=(act == "h" and g == PASSES - 1),
-                        )
-            for bt in range(BATCH_TILES):
-                z_in = work.tile([P, HALF], F32, name="z_in")
-                nc.vector.tensor_tensor(out=z_in[:], in0=banks[bt][:], in1=bias_z[:, cols], op=ALU.add)
-                nc.scalar.activation(out=z[:, bt, cols], in_=z_in[:], func=ACT.Sigmoid)
-                nc.gpsimd.tensor_tensor(out=zh[:, bt, cols], in0=z[:, bt, cols], in1=rows["h"][:, bt, cols], op=ALU.mult)
+            z_in = work.tile([P, HALF], F32, name="z_in")
+            nc.vector.tensor_tensor(out=z_in[:], in0=z_banks[half, bt][:], in1=bias_z[:, cols], op=ALU.add)
+            nc.scalar.activation(out=z[:, bt, cols], in_=z_in[:], func=ACT.Sigmoid)
+            nc.gpsimd.tensor_tensor(out=zh[:, bt, cols], in0=z[:, bt, cols], in1=rows["h"][:, bt, cols], op=ALU.mult)
 
-        z_products(0)
+        for bt in range(BATCH_TILES):
+            transpose_pairs(bt, "x", bt)
+            if bt > 0:
+                quantise("x", bt - 1)
+        quantise("x", BATCH_TILES - 1)
+        for pair in range(BATCH_TILES // 2):
+            first, second = 2 * pair, 2 * pair + 1
+            z_passes("x", "Wiz", 0, first)
+            z_passes("x", "Wiz", 0, second)
+            transpose_pairs(first, "h", first)
+            transpose_pairs(second, "h", second)
+            quantise("h", first)
+            quantise("h", second)
+        for half in range(HALVES):
+            spread_bias_z(half)
+        for bt in range(BATCH_TILES):
+            z_passes("h", "Whz", 0, bt)
+            finish_z(0, bt)
 
         bias_bank = psum.tile([P, P], BF16, name="bias_bank", tag="bank")
         nc.tensor.transpose(bias_bank[:], bias_n_rows[:], ident_bf16[:])
@@ -230,7 +238,11 @@ def tile_gru_kernel(
         bias_hn = bias_cols[:, 2 * FEATURE_TILES : 3 * FEATURE_TILES]
         bias_in = bias_cols[:, 3 * FEATURE_TILES : 4 * FEATURE_TILES]
 
-        z_products(1)
+        for bt in range(BATCH_TILES):
+            z_passes("x", "Wiz", 1, bt)
+        for bt in range(BATCH_TILES):
+            z_passes("h", "Whz", 1, bt)
+            finish_z(1, bt)
 
         def product(label, pairs, m, batch):
             half, tile_in_half = divmod(m, HALF // P)
@@ -274,7 +286,7 @@ def tile_gru_kernel(
 
         out_view = out.rearrange("(t b) n -> b t n", b=P)
 
-        def blend(m, tiles, adder):
+        def blend(m, tiles):
             cols = slice(P * m, P * (m + 1))
             span = slice(tiles.start, tiles.stop)
             bank = psum.tile([P, len(tiles), P], F32, name="n_T", tag="bank")
@@ -282,27 +294,34 @@ def tile_gru_kernel(
                 nc.tensor.transpose(bank[:, index, :], n[m][:, P * bt : P * (bt + 1)], ident_f32[:])
             part = work.tile([P, len(tiles), P], F32, name="part")
             nc.vector.scalar_tensor_tensor(out=part[:], in0=z[:, span, cols], scalar=1.0, in1=bank[:], op0=ALU.subtract, op1=ALU.mult)
-            res = work.tile([P, len(tiles), P], F32, name="res")
-            adder.tensor_tensor(out=res[:], in0=zh[:, span, cols], in1=part[:], op=ALU.subtract)
-            nc.sync.dma_start(out=out_view[:, span, cols], in_=res[:])
+
+            def finish(adder):
+                res = work.tile([P, len(tiles), P], F32, name="res")
+                adder.tensor_tensor(out=res[:], in0=zh[:, span, cols], in1=part[:], op=ALU.subtract)
+                nc.sync.dma_start(out=out_view[:, span, cols], in_=res[:])
+
+            return finish
 
         all_tiles = range(BATCH_TILES)
         last = FEATURE_TILES - 1
-        blended_in_turn = {3: (0, 1), 5: (2, 3), 6: (4,)}
         make_r(0)
         for turn in range(last):
-            make_r(turn + 1)
+            if turn + 1 < last:
+                make_r(turn + 1)
             make_rh(turn, whole)
             if turn > 0:
                 make_n(turn - 1, whole)
-            for m in blended_in_turn.get(turn, ()):
-                blend(m, all_tiles, nc.gpsimd)
+            blended = {3: (0, 1), 5: (2, 3), 6: (4,)}.get(turn, ())
+            for m in blended:
+                blend(m, all_tiles)(nc.gpsimd)
         halves = [range(0, BATCH_TILES // 2), range(BATCH_TILES // 2, BATCH_TILES)]
-        make_rh(last, whole)
+        make_r(last)
         make_n(last - 1, whole)
-        blend(last - 2, all_tiles, nc.gpsimd)
+        make_rh(last, whole)
+        blend(last - 2, all_tiles)(nc.gpsimd)
         for tiles in halves:
             make_n(last, slice(P * tiles.start, P * tiles.stop))
-        blend(last - 1, all_tiles, nc.gpsimd)
-        for tiles in halves:
-            blend(last, tiles, nc.vector)
+        blend(last - 1, all_tiles)(nc.gpsimd)
+        finishes = [blend(last, tiles) for tiles in halves]
+        for finish in finishes:
+            finish(nc.vector)

@@ -201,12 +201,17 @@ def tile_gru_kernel(
                     stop=(act == "h" and g == PASSES - 1),
                 )
 
-        def finish_z(half, bt):
+        def finish_z(half, bt, multiplier):
             cols = slice(HALF * half, HALF * (half + 1))
             z_in = work.tile([P, HALF], F32, name="z_in")
             nc.vector.tensor_tensor(out=z_in[:], in0=z_banks[half, bt][:], in1=bias_z[:, cols], op=ALU.add)
             nc.scalar.activation(out=z[:, bt, cols], in_=z_in[:], func=ACT.Sigmoid)
-            nc.gpsimd.tensor_tensor(out=zh[:, bt, cols], in0=z[:, bt, cols], in1=rows["h"][:, bt, cols], op=ALU.mult)
+            if multiplier is not None:
+                z_times_hidden(half, bt, multiplier)
+
+        def z_times_hidden(half, bt, multiplier):
+            cols = slice(HALF * half, HALF * (half + 1))
+            multiplier.tensor_tensor(out=zh[:, bt, cols], in0=z[:, bt, cols], in1=rows["h"][:, bt, cols], op=ALU.mult)
 
         for bt in range(BATCH_TILES):
             transpose_pairs(bt, "x", bt)
@@ -225,7 +230,7 @@ def tile_gru_kernel(
             spread_bias_z(half)
         for bt in range(BATCH_TILES):
             z_passes("h", "Whz", 0, bt)
-            finish_z(0, bt)
+            finish_z(0, bt, nc.gpsimd)
 
         bias_bank = psum.tile([P, P], BF16, name="bias_bank", tag="bank")
         nc.tensor.transpose(bias_bank[:], bias_n_rows[:], ident_bf16[:])
@@ -242,7 +247,9 @@ def tile_gru_kernel(
             z_passes("x", "Wiz", 1, bt)
         for bt in range(BATCH_TILES):
             z_passes("h", "Whz", 1, bt)
-            finish_z(1, bt)
+            finish_z(1, bt, None)
+        for bt in range(BATCH_TILES):
+            z_times_hidden(1, bt, nc.vector)
 
         def product(label, pairs, m, batch):
             half, tile_in_half = divmod(m, HALF // P)
@@ -267,7 +274,7 @@ def tile_gru_kernel(
 
         def make_r(m):
             bank = product("r", (("x", "Wir"), ("h", "Whr")), m, whole)
-            r[m] = work.tile([P, BATCH], F32, name="r")
+            r[m] = keep.tile([P, BATCH], F32, name="r_%d" % m)
             nc.scalar.activation(out=r[m][:], in_=bank[:], func=ACT.Sigmoid, bias=bias_r[:, m : m + 1])
             rh[m] = work.tile([P, BATCH], F32, name="rh")
             n[m] = work.tile([P, BATCH], F32, name="n")
@@ -304,10 +311,11 @@ def tile_gru_kernel(
 
         all_tiles = range(BATCH_TILES)
         last = FEATURE_TILES - 1
-        make_r(0)
+        for m in range(4):
+            make_r(m)
         for turn in range(last):
-            if turn + 1 < last:
-                make_r(turn + 1)
+            if turn in (1, 3, 5):
+                make_r(4 + turn // 2)
             make_rh(turn, whole)
             if turn > 0:
                 make_n(turn - 1, whole)

@@ -65,6 +65,14 @@ def tile_gru_kernel(
         ident_f32 = keep.tile([P, P], F32, name="ident_f32")
         make_identity(nc, ident_f32[:])
 
+        zeros = keep.tile([P, HALF], BF16, name="zeros")
+        nc.vector.memset(zeros[:].bitcast(I32), 0)
+        idle_bank = psum.tile([P, HALF], F32, name="idle_bank", tag="bank")
+
+        def keep_clock(count):
+            for turn in range(count):
+                nc.tensor.matmul(idle_bank[:], lhsT=zeros[:, 0:P], rhs=zeros[:], start=True, stop=True)
+
         zero_col = keep.tile([P, 1], F32, name="zero_col")
         nc.vector.memset(zero_col[:], 0.0)
         warm_col = keep.tile([P, 1], F32, name="warm_col")
@@ -213,8 +221,10 @@ def tile_gru_kernel(
             cols = slice(HALF * half, HALF * (half + 1))
             multiplier.tensor_tensor(out=zh[:, bt, cols], in0=z[:, bt, cols], in1=rows["h"][:, bt, cols], op=ALU.mult)
 
+        keep_clock(5)
         for bt in range(BATCH_TILES):
             transpose_pairs(bt, "x", bt)
+            keep_clock(1)
             if bt > 0:
                 quantise("x", bt - 1)
         quantise("x", BATCH_TILES - 1)

@@ -158,17 +158,29 @@ def tile_gru_kernel(
         codes = {}
         act_planes = {}
         for act in ("x", "h"):
-            grouped[act] = keep.tile([P, PASSES, 4 * BATCH], BF16, name="grouped_" + act, align_bytes=64)
+            for bt in range(BATCH_TILES):
+                grouped[act, bt] = keep.tile([P, PASSES, 4 * P], BF16, name="grouped_%s_%d" % (act, bt), align_bytes=64)
             codes[act] = keep.tile([P, PASSES, BATCH], U32, name="codes_" + act, align_bytes=64)
             act_planes[act] = keep.tile([P, PASSES, BATCH], U8, name="act_planes_" + act, align_bytes=64)
 
+        sorted_h = keep.tile([P, BATCH_TILES, PASSES, 2, P], F32, name="sorted_h")
+
+        def sort_hidden(bt):
+            nc.scalar.copy(
+                out=sorted_h[:, bt, :, :, :],
+                in_=rows["h"][:, bt, :].bitcast(F32).rearrange("b (g p u) -> b g u p", g=PASSES, u=2),
+            )
+
         def transpose_pairs(index, act, bt):
-            pairs = rows[act][:, bt, :].bitcast(F32)
             bank = psum.tile([P, PASSES, 2, P], F32, name="pairs_T", tag="bank")
             for g in range(PASSES):
                 for u in range(2):
-                    nc.tensor.transpose(bank[:, g, u, :], pairs[:, 256 * g + u : 256 * (g + 1) : 2], ident_f32[:])
-            target = grouped[act][:].bitcast(F32).rearrange("p g (b u) -> p g b u", u=2)[:, :, P * bt : P * (bt + 1), :]
+                    if act == "x":
+                        source = rows["x"][:, bt, :].bitcast(F32)[:, 256 * g + u : 256 * (g + 1) : 2]
+                    else:
+                        source = sorted_h[:, bt, g, u, :]
+                    nc.tensor.transpose(bank[:, g, u, :], source, ident_f32[:])
+            target = grouped[act, bt][:].bitcast(F32).rearrange("p g (b u) -> p g b u", u=2)
             source = bank[:].rearrange("p g u b -> p g b u")
             if index % 2 == 0:
                 nc.vector.tensor_copy(out=target, in_=source)
@@ -180,7 +192,7 @@ def tile_gru_kernel(
                 nc.vector.quantize_mx(
                     out=codes[act][:, g, P * bt : P * (bt + 1)].bitcast(FP8X4),
                     scales=act_planes[act][:, g, P * bt : P * (bt + 1)],
-                    in_=grouped[act][:, g, 4 * P * bt : 4 * P * (bt + 1)],
+                    in_=grouped[act, bt][:, g, :],
                 )
 
         bias_z = keep.tile([P, FEATURES], F32, name="bias_z")
@@ -228,14 +240,15 @@ def tile_gru_kernel(
             if bt > 0:
                 quantise("x", bt - 1)
         quantise("x", BATCH_TILES - 1)
-        for pair in range(BATCH_TILES // 2):
-            first, second = 2 * pair, 2 * pair + 1
-            z_passes("x", "Wiz", 0, first)
-            z_passes("x", "Wiz", 0, second)
-            transpose_pairs(first, "h", first)
-            transpose_pairs(second, "h", second)
-            quantise("h", first)
-            quantise("h", second)
+        for bt in range(BATCH_TILES):
+            sort_hidden(bt)
+        for bt in range(BATCH_TILES):
+            z_passes("x", "Wiz", 0, bt)
+        for bt in range(BATCH_TILES):
+            transpose_pairs(bt, "h", bt)
+            if bt > 0:
+                quantise("h", bt - 1)
+        quantise("h", BATCH_TILES - 1)
         for half in range(HALVES):
             spread_bias_z(half)
         for bt in range(BATCH_TILES):

@@ -85,7 +85,7 @@ def tile_gru_kernel(
         planes = {}
 
         def clear_planes(name):
-            planes[name] = keep.tile([P, FEATURES], U8, name="planes_" + name, align_bytes=64)
+            planes[name] = keep.tile([P, FEATURES], U8, name="planes_" + name, align_bytes=256)
             nc.vector.memset(planes[name][:].bitcast(I32), 0)
 
         clear_planes("Wiz")
@@ -110,7 +110,7 @@ def tile_gru_kernel(
         words = {}
 
         def load_words(name, half):
-            words[name, half] = keep.tile([P, PASSES, HALF], I32, name="words_%s_%d" % (name, half), align_bytes=64)
+            words[name, half] = keep.tile([P, PASSES, HALF], I32, name="words_%s_%d" % (name, half), align_bytes=256)
             source = dram_words[name].rearrange("g p n t -> p g (n t)")
             nc.sync.dma_start(
                 out=words[name, half][:],
@@ -159,9 +159,9 @@ def tile_gru_kernel(
         act_planes = {}
         for act in ("x", "h"):
             for bt in range(BATCH_TILES):
-                grouped[act, bt] = keep.tile([P, PASSES, 4 * P], BF16, name="grouped_%s_%d" % (act, bt), align_bytes=64)
-            codes[act] = keep.tile([P, PASSES, BATCH], U32, name="codes_" + act, align_bytes=64)
-            act_planes[act] = keep.tile([P, PASSES, BATCH], U8, name="act_planes_" + act, align_bytes=64)
+                grouped[act, bt] = keep.tile([P, PASSES, 4 * P], BF16, name="grouped_%s_%d" % (act, bt), align_bytes=256)
+            codes[act] = keep.tile([P, PASSES, BATCH], U32, name="codes_" + act, align_bytes=256)
+            act_planes[act] = keep.tile([P, PASSES, BATCH], U8, name="act_planes_" + act, align_bytes=256)
 
         sorted_h = keep.tile([P, BATCH_TILES, PASSES, 2, P], F32, name="sorted_h")
 

@@ -62,10 +62,10 @@ def tile_gru_kernel(
         work = stack.enter_context(tc.tile_pool(name="work", bufs=4))
         psum = stack.enter_context(tc.psum_pool(name="psum", bufs=8))
 
-        ident_f32 = keep.tile([P, P], F32, name="ident_f32")
+        ident_f32 = keep.tile([P, P], F32, name="ident_f32", align_bytes=256)
         make_identity(nc, ident_f32[:])
 
-        zeros = keep.tile([P, HALF], BF16, name="zeros")
+        zeros = keep.tile([P, HALF], BF16, name="zeros", align_bytes=256)
         nc.vector.memset(zeros[:].bitcast(I32), 0)
         idle_bank = psum.tile([P, HALF], F32, name="idle_bank", tag="bank")
 
@@ -78,9 +78,9 @@ def tile_gru_kernel(
         warm_col = keep.tile([P, 1], F32, name="warm_col")
         nc.scalar.activation(out=warm_col[:], in_=zero_col[:], func=ACT.Sigmoid)
 
-        bias_z_rows = keep.tile([P, FEATURES], BF16, name="bias_z_rows")
+        bias_z_rows = keep.tile([P, FEATURES], BF16, name="bias_z_rows", align_bytes=256)
         nc.vector.memset(bias_z_rows[:].bitcast(I32), 0)
-        bias_n_rows = keep.tile([P, P], BF16, name="bias_n_rows")
+        bias_n_rows = keep.tile([P, P], BF16, name="bias_n_rows", align_bytes=256)
         nc.vector.memset(bias_n_rows[:].bitcast(I32), 0)
         planes = {}
 
@@ -90,10 +90,10 @@ def tile_gru_kernel(
 
         clear_planes("Wiz")
         clear_planes("Whz")
-        add_rows = keep.tile([P, P], BF16, name="add_rows")
+        add_rows = keep.tile([P, P], BF16, name="add_rows", align_bytes=256)
         nc.vector.memset(add_rows[:], 0.0)
         nc.vector.memset(add_rows[0:2, :], 1.0)
-        ident_bf16 = keep.tile([P, P], BF16, name="ident_bf16")
+        ident_bf16 = keep.tile([P, P], BF16, name="ident_bf16", align_bytes=256)
         nc.vector.tensor_copy(out=ident_bf16[:], in_=ident_f32[:])
         for name in ("Wir", "Whr", "Whn", "Win"):
             clear_planes(name)
@@ -101,7 +101,7 @@ def tile_gru_kernel(
 
         rows = {}
         for act in ("x", "h"):
-            rows[act] = keep.tile([P, BATCH_TILES, K], BF16, name="rows_" + act)
+            rows[act] = keep.tile([P, BATCH_TILES, K], BF16, name="rows_" + act, align_bytes=256)
 
         def load_rows(act, first, last):
             source = dram_rows[act].rearrange("(t b) k -> b t k", b=P)
@@ -163,7 +163,7 @@ def tile_gru_kernel(
             codes[act] = keep.tile([P, PASSES, BATCH], U32, name="codes_" + act, align_bytes=256)
             act_planes[act] = keep.tile([P, PASSES, BATCH], U8, name="act_planes_" + act, align_bytes=256)
 
-        sorted_h = keep.tile([P, BATCH_TILES, PASSES, 2, P], F32, name="sorted_h")
+        sorted_h = keep.tile([P, BATCH_TILES, PASSES, 2, P], F32, name="sorted_h", align_bytes=256)
 
         def sort_hidden(bt):
             nc.scalar.copy(
@@ -195,9 +195,9 @@ def tile_gru_kernel(
                     in_=grouped[act, bt][:, g, :],
                 )
 
-        bias_z = keep.tile([P, FEATURES], F32, name="bias_z")
-        z = keep.tile([P, BATCH_TILES, FEATURES], F32, name="z")
-        zh = keep.tile([P, BATCH_TILES, FEATURES], F32, name="zh")
+        bias_z = keep.tile([P, FEATURES], F32, name="bias_z", align_bytes=256)
+        z = keep.tile([P, BATCH_TILES, FEATURES], F32, name="z", align_bytes=256)
+        zh = keep.tile([P, BATCH_TILES, FEATURES], F32, name="zh", align_bytes=256)
         z_banks = {}
 
         def spread_bias_z(half):
@@ -223,7 +223,7 @@ def tile_gru_kernel(
 
         def finish_z(half, bt, multiplier):
             cols = slice(HALF * half, HALF * (half + 1))
-            z_in = work.tile([P, HALF], F32, name="z_in")
+            z_in = work.tile([P, HALF], F32, name="z_in", align_bytes=256)
             nc.vector.tensor_tensor(out=z_in[:], in0=z_banks[half, bt][:], in1=bias_z[:, cols], op=ALU.add)
             nc.scalar.activation(out=z[:, bt, cols], in_=z_in[:], func=ACT.Sigmoid)
             if multiplier is not None:
@@ -297,10 +297,10 @@ def tile_gru_kernel(
 
         def make_r(m):
             bank = product("r", (("x", "Wir"), ("h", "Whr")), m, whole)
-            r[m] = keep.tile([P, BATCH], F32, name="r_%d" % m)
+            r[m] = keep.tile([P, BATCH], F32, name="r_%d" % m, align_bytes=256)
             nc.scalar.activation(out=r[m][:], in_=bank[:], func=ACT.Sigmoid, bias=bias_r[:, m : m + 1])
-            rh[m] = work.tile([P, BATCH], F32, name="rh")
-            n[m] = work.tile([P, BATCH], F32, name="n")
+            rh[m] = work.tile([P, BATCH], F32, name="rh", align_bytes=256)
+            n[m] = work.tile([P, BATCH], F32, name="n", align_bytes=256)
 
         def make_rh(m, batch):
             bank = product("hn", (("h", "Whn"),), m, batch)
@@ -310,7 +310,7 @@ def tile_gru_kernel(
 
         def make_n(m, batch):
             bank = product("in", (("x", "Win"),), m, batch)
-            n_in = work.tile([P, batch.stop - batch.start], F32, name="n_in")
+            n_in = work.tile([P, batch.stop - batch.start], F32, name="n_in", align_bytes=256)
             nc.vector.tensor_tensor(out=n_in[:], in0=bank[:], in1=rh[m][:, batch], op=ALU.add)
             nc.scalar.activation(out=n[m][:, batch], in_=n_in[:], func=ACT.Tanh, bias=bias_in[:, m : m + 1])
 
@@ -322,11 +322,11 @@ def tile_gru_kernel(
             bank = psum.tile([P, len(tiles), P], F32, name="n_T", tag="bank")
             for index, bt in enumerate(tiles):
                 nc.tensor.transpose(bank[:, index, :], n[m][:, P * bt : P * (bt + 1)], ident_f32[:])
-            part = work.tile([P, len(tiles), P], F32, name="part")
+            part = work.tile([P, len(tiles), P], F32, name="part", align_bytes=256)
             nc.vector.scalar_tensor_tensor(out=part[:], in0=z[:, span, cols], scalar=1.0, in1=bank[:], op0=ALU.subtract, op1=ALU.mult)
 
             def finish(adder):
-                res = work.tile([P, len(tiles), P], F32, name="res")
+                res = work.tile([P, len(tiles), P], F32, name="res", align_bytes=256)
                 adder.tensor_tensor(out=res[:], in0=zh[:, span, cols], in1=part[:], op=ALU.subtract)
                 nc.sync.dma_start(out=out_view[:, span, cols], in_=res[:])
 

@@ -60,6 +60,7 @@ def tile_gru_kernel(
         stack.enter_context(tc.manual_schedule())
         keep = stack.enter_context(tc.tile_pool(name="keep", bufs=1))
         work = stack.enter_context(tc.tile_pool(name="work", bufs=4))
+        results = stack.enter_context(tc.tile_pool(name="results", bufs=8))
         psum = stack.enter_context(tc.psum_pool(name="psum", bufs=8))
 
         ident_f32 = keep.tile([P, P], F32, name="ident_f32", align_bytes=256)
@@ -67,9 +68,9 @@ def tile_gru_kernel(
 
         zeros = keep.tile([P, HALF], BF16, name="zeros", align_bytes=256)
         nc.vector.memset(zeros[:].bitcast(I32), 0)
-        idle_bank = psum.tile([P, HALF], F32, name="idle_bank", tag="bank")
 
         def keep_clock(count):
+            idle_bank = psum.tile([P, HALF], F32, name="idle_bank", tag="bank")
             for turn in range(count):
                 nc.tensor.matmul(idle_bank[:], lhsT=zeros[:, 0:P], rhs=zeros[:], start=True, stop=True)
 
@@ -89,15 +90,15 @@ def tile_gru_kernel(
             nc.vector.memset(planes[name][:].bitcast(I32), 0)
 
         clear_planes("Wiz")
+        clear_planes("Win")
         clear_planes("Whz")
         add_rows = keep.tile([P, P], BF16, name="add_rows", align_bytes=256)
         nc.vector.memset(add_rows[:], 0.0)
         nc.vector.memset(add_rows[0:2, :], 1.0)
         ident_bf16 = keep.tile([P, P], BF16, name="ident_bf16", align_bytes=256)
         nc.vector.tensor_copy(out=ident_bf16[:], in_=ident_f32[:])
-        for name in ("Wir", "Whr", "Whn", "Win"):
+        for name in ("Wir", "Whr", "Whn"):
             clear_planes(name)
-
 
         rows = {}
         for act in ("x", "h"):
@@ -124,13 +125,13 @@ def tile_gru_kernel(
                     in_=dram_scales[name][:, 4 * quadrant : 4 * quadrant + 4, :].bitcast(I32),
                 )
 
-        for row, name in enumerate(("Wiz", "Whz")):
-            nc.gpsimd.dma_start(out=bias_z_rows[row : row + 1, :], in_=dram_bias[name].rearrange("(o n) -> o n", o=1))
         for index, name in enumerate(("Wir", "Whr", "Whn", "Win")):
             nc.gpsimd.dma_start(
                 out=bias_n_rows[FEATURE_TILES * index : FEATURE_TILES * (index + 1), :],
                 in_=dram_bias[name].rearrange("(m j) -> m j", j=P),
             )
+        for row, name in enumerate(("Wiz", "Whz")):
+            nc.gpsimd.dma_start(out=bias_z_rows[row : row + 1, :], in_=dram_bias[name].rearrange("(o n) -> o n", o=1))
 
         load_rows("x", 0, 1)
         load_rows("x", 1, 2)
@@ -139,19 +140,10 @@ def tile_gru_kernel(
         load_words("Wiz", 0)
         load_rows("h", 0, 2)
         load_rows("h", 2, 4)
-        load_words("Whz", 0)
-        load_scales("Whz")
-        load_words("Wiz", 1)
-        load_scales("Wir")
-        load_words("Whz", 1)
-        load_scales("Whr")
-        load_words("Wir", 0)
-        load_scales("Whn")
-        load_words("Whr", 0)
-        load_scales("Win")
-        load_words("Whn", 0)
-        load_words("Win", 0)
-        for name in ("Wir", "Whr", "Whn", "Win"):
+        for name in ("Win", "Whz", "Wir", "Whr", "Whn"):
+            load_words(name, 0)
+            load_scales(name)
+        for name in ("Wiz", "Whz", "Wir", "Whr", "Whn", "Win"):
             load_words(name, 1)
 
         grouped = {}
@@ -165,35 +157,43 @@ def tile_gru_kernel(
 
         sorted_h = keep.tile([P, BATCH_TILES, PASSES, 2, P], F32, name="sorted_h", align_bytes=256)
 
-        def sort_hidden(bt):
-            nc.scalar.copy(
+        def sort_hidden(bt, copy):
+            copy(
                 out=sorted_h[:, bt, :, :, :],
                 in_=rows["h"][:, bt, :].bitcast(F32).rearrange("b (g p u) -> b g u p", g=PASSES, u=2),
             )
 
-        def transpose_pairs(index, act, bt):
-            bank = psum.tile([P, PASSES, 2, P], F32, name="pairs_T", tag="bank")
+        def transpose_x(bt, g, copy):
+            bank = psum.tile([P, 2, P], F32, name="x_T", tag="bank")
+            for u in range(2):
+                source = rows["x"][:, bt, :].bitcast(F32)[:, 256 * g + u : 256 * (g + 1) : 2]
+                nc.tensor.transpose(bank[:, u, :], source, ident_f32[:])
+            copy(
+                out=grouped["x", bt][:, g, :].bitcast(F32).rearrange("p (b u) -> p b u", u=2),
+                in_=bank[:].rearrange("p u b -> p b u"),
+            )
+
+        def transpose_h(bt):
+            bank = psum.tile([P, PASSES, 2, P], F32, name="h_T", tag="bank")
             for g in range(PASSES):
                 for u in range(2):
-                    if act == "x":
-                        source = rows["x"][:, bt, :].bitcast(F32)[:, 256 * g + u : 256 * (g + 1) : 2]
-                    else:
-                        source = sorted_h[:, bt, g, u, :]
-                    nc.tensor.transpose(bank[:, g, u, :], source, ident_f32[:])
-            target = grouped[act, bt][:].bitcast(F32).rearrange("p g (b u) -> p g b u", u=2)
-            source = bank[:].rearrange("p g u b -> p g b u")
-            if index % 2 == 0:
-                nc.vector.tensor_copy(out=target, in_=source)
-            else:
-                nc.scalar.copy(out=target, in_=source)
+                    nc.tensor.transpose(bank[:, g, u, :], sorted_h[:, bt, g, u, :], ident_f32[:])
+            copy = nc.scalar.copy if bt % 2 else nc.vector.tensor_copy
+            copy(
+                out=grouped["h", bt][:].bitcast(F32).rearrange("p g (b u) -> p g b u", u=2),
+                in_=bank[:].rearrange("p g u b -> p g b u"),
+            )
+
+        def quantise_pass(act, bt, g):
+            nc.vector.quantize_mx(
+                out=codes[act][:, g, P * bt : P * (bt + 1)].bitcast(FP8X4),
+                scales=act_planes[act][:, g, P * bt : P * (bt + 1)],
+                in_=grouped[act, bt][:, g, :],
+            )
 
         def quantise(act, bt):
             for g in range(PASSES):
-                nc.vector.quantize_mx(
-                    out=codes[act][:, g, P * bt : P * (bt + 1)].bitcast(FP8X4),
-                    scales=act_planes[act][:, g, P * bt : P * (bt + 1)],
-                    in_=grouped[act, bt][:, g, :],
-                )
+                quantise_pass(act, bt, g)
 
         bias_z = keep.tile([P, FEATURES], F32, name="bias_z", align_bytes=256)
         z = keep.tile([P, BATCH_TILES, FEATURES], F32, name="z", align_bytes=256)
@@ -233,74 +233,50 @@ def tile_gru_kernel(
             cols = slice(HALF * half, HALF * (half + 1))
             multiplier.tensor_tensor(out=zh[:, bt, cols], in0=z[:, bt, cols], in1=rows["h"][:, bt, cols], op=ALU.mult)
 
-        keep_clock(5)
-        for bt in range(BATCH_TILES):
-            transpose_pairs(bt, "x", bt)
-            keep_clock(1)
-            if bt > 0:
-                quantise("x", bt - 1)
-        quantise("x", BATCH_TILES - 1)
-        for bt in range(BATCH_TILES):
-            sort_hidden(bt)
-        for bt in range(BATCH_TILES):
-            z_passes("x", "Wiz", 0, bt)
-        for bt in range(BATCH_TILES):
-            transpose_pairs(bt, "h", bt)
-            if bt > 0:
-                quantise("h", bt - 1)
-        quantise("h", BATCH_TILES - 1)
-        for half in range(HALVES):
-            spread_bias_z(half)
-        for bt in range(BATCH_TILES):
-            z_passes("h", "Whz", 0, bt)
-            finish_z(0, bt, nc.gpsimd)
-
-        bias_bank = psum.tile([P, P], BF16, name="bias_bank", tag="bank")
-        nc.tensor.transpose(bias_bank[:], bias_n_rows[:], ident_bf16[:])
-        bias_cols = keep.tile([P, 4 * FEATURE_TILES], F32, name="bias_cols")
-        nc.vector.tensor_copy(out=bias_cols[:], in_=bias_bank[:, 0 : 4 * FEATURE_TILES])
-        bias_r = keep.tile([P, FEATURE_TILES], F32, name="bias_r")
-        nc.vector.tensor_tensor(
-            out=bias_r[:], in0=bias_cols[:, 0:FEATURE_TILES], in1=bias_cols[:, FEATURE_TILES : 2 * FEATURE_TILES], op=ALU.add
-        )
-        bias_hn = bias_cols[:, 2 * FEATURE_TILES : 3 * FEATURE_TILES]
-        bias_in = bias_cols[:, 3 * FEATURE_TILES : 4 * FEATURE_TILES]
-
-        for bt in range(BATCH_TILES):
-            z_passes("x", "Wiz", 1, bt)
-        for bt in range(BATCH_TILES):
-            z_passes("h", "Whz", 1, bt)
-            finish_z(1, bt, None)
-        for bt in range(BATCH_TILES):
-            z_times_hidden(1, bt, nc.vector)
-
-        def product(label, pairs, m, batch):
+        def one_pass(bank, act, name, m, batch, g, start, stop):
             half, tile_in_half = divmod(m, HALF // P)
-            bank = psum.tile([P, batch.stop - batch.start], F32, name="bank_" + label, tag="bank")
+            nc.tensor.matmul_mx(
+                out=bank[:],
+                lhsT=words[name, half][:, g, P * tile_in_half : P * (tile_in_half + 1)].bitcast(FP8X4),
+                lhsT_scale=planes[name][4 * g : P, P * m : P * (m + 1)],
+                rhs=codes[act][:, g, batch].bitcast(FP8X4),
+                rhs_scale=act_planes[act][:, g, batch],
+                start=start,
+                stop=stop,
+            )
+
+        def passes(bank, pairs, m, batch, first=True, final=True):
             steps = [(act, name, g) for act, name in pairs for g in range(PASSES)]
             for step, (act, name, g) in enumerate(steps):
-                nc.tensor.matmul_mx(
-                    out=bank[:],
-                    lhsT=words[name, half][:, g, P * tile_in_half : P * (tile_in_half + 1)].bitcast(FP8X4),
-                    lhsT_scale=planes[name][4 * g : P, P * m : P * (m + 1)],
-                    rhs=codes[act][:, g, batch].bitcast(FP8X4),
-                    rhs_scale=act_planes[act][:, g, batch],
-                    start=(step == 0),
-                    stop=(step == len(steps) - 1),
-                )
+                one_pass(bank, act, name, m, batch, g, first and step == 0, final and step == len(steps) - 1)
+
+        def product(label, pairs, m, batch):
+            bank = psum.tile([P, batch.stop - batch.start], F32, name="bank_" + label, tag="bank")
+            passes(bank, pairs, m, batch)
             return bank
+
+        whole = slice(0, BATCH)
+        x_in = {}
 
         r = {}
         rh = {}
         n = {}
-        whole = slice(0, BATCH)
+
+        r_banks = {}
+
+        def open_r(m):
+            r_banks[m] = psum.tile([P, BATCH], F32, name="bank_r", tag="bank")
+            passes(r_banks[m], (("x", "Wir"),), m, whole, final=False)
 
         def make_r(m):
-            bank = product("r", (("x", "Wir"), ("h", "Whr")), m, whole)
-            r[m] = keep.tile([P, BATCH], F32, name="r_%d" % m, align_bytes=256)
+            if m not in r_banks:
+                open_r(m)
+            bank = r_banks[m]
+            passes(bank, (("h", "Whr"),), m, whole, first=False)
+            r[m] = work.tile([P, BATCH], F32, name="r", align_bytes=256)
             nc.scalar.activation(out=r[m][:], in_=bank[:], func=ACT.Sigmoid, bias=bias_r[:, m : m + 1])
             rh[m] = work.tile([P, BATCH], F32, name="rh", align_bytes=256)
-            n[m] = work.tile([P, BATCH], F32, name="n", align_bytes=256)
+            n[m] = keep.tile([P, BATCH], F32, name="n_%d" % m, align_bytes=256)
 
         def make_rh(m, batch):
             bank = product("hn", (("h", "Whn"),), m, batch)
@@ -308,25 +284,33 @@ def tile_gru_kernel(
                 out=rh[m][:, batch], in0=bank[:], scalar=bias_hn[:, m : m + 1], in1=r[m][:, batch], op0=ALU.add, op1=ALU.mult
             )
 
-        def make_n(m, batch):
-            bank = product("in", (("x", "Win"),), m, batch)
+        def make_x_in(m):
+            bank = product("x_in", (("x", "Win"),), m, whole)
+            x_in[m] = keep.tile([P, BATCH], F32, name="x_in_%d" % m, align_bytes=256)
+            nc.scalar.copy(out=x_in[m][:], in_=bank[:])
+
+        def make_n(m, batch, adder):
+            bank = x_in[m][:, batch] if m in x_in else product("in", (("x", "Win"),), m, batch)[:]
             n_in = work.tile([P, batch.stop - batch.start], F32, name="n_in", align_bytes=256)
-            nc.vector.tensor_tensor(out=n_in[:], in0=bank[:], in1=rh[m][:, batch], op=ALU.add)
+            adder.tensor_tensor(out=n_in[:], in0=bank, in1=rh[m][:, batch], op=ALU.add)
             nc.scalar.activation(out=n[m][:, batch], in_=n_in[:], func=ACT.Tanh, bias=bias_in[:, m : m + 1])
 
         out_view = out.rearrange("(t b) n -> b t n", b=P)
 
-        def blend(m, tiles):
-            cols = slice(P * m, P * (m + 1))
-            span = slice(tiles.start, tiles.stop)
+        def turn_n(m, tiles):
             bank = psum.tile([P, len(tiles), P], F32, name="n_T", tag="bank")
             for index, bt in enumerate(tiles):
                 nc.tensor.transpose(bank[:, index, :], n[m][:, P * bt : P * (bt + 1)], ident_f32[:])
+            return bank
+
+        def blend(m, tiles, bank):
+            cols = slice(P * m, P * (m + 1))
+            span = slice(tiles.start, tiles.stop)
             part = work.tile([P, len(tiles), P], F32, name="part", align_bytes=256)
             nc.vector.scalar_tensor_tensor(out=part[:], in0=z[:, span, cols], scalar=1.0, in1=bank[:], op0=ALU.subtract, op1=ALU.mult)
 
             def finish(adder):
-                res = work.tile([P, len(tiles), P], F32, name="res", align_bytes=256)
+                res = results.tile([P, len(tiles), P], F32, name="res", align_bytes=256)
                 adder.tensor_tensor(out=res[:], in0=zh[:, span, cols], in1=part[:], op=ALU.subtract)
                 nc.sync.dma_start(out=out_view[:, span, cols], in_=res[:])
 
@@ -334,25 +318,102 @@ def tile_gru_kernel(
 
         all_tiles = range(BATCH_TILES)
         last = FEATURE_TILES - 1
+
+        def make_z(index):
+            half, bt = divmod(index, BATCH_TILES)
+            if (half, bt) not in z_banks:
+                z_passes("x", "Wiz", half, bt)
+            z_passes("h", "Whz", half, bt)
+            finish_z(half, bt, nc.gpsimd)
+
+        copies = (nc.vector.tensor_copy, nc.scalar.copy)
+        keep_clock(4)
+        for bt in range(BATCH_TILES):
+            for g in range(PASSES):
+                transpose_x(bt, g, copies[g])
+            if bt == 1:
+                keep_clock(2)
+            if bt > 0:
+                quantise("x", bt - 1)
+        quantise("x", BATCH_TILES - 1)
+        for bt in range(BATCH_TILES):
+            z_passes("x", "Wiz", 0, bt)
+        for bt in range(BATCH_TILES):
+            sort_hidden(bt, copies[(bt + 1) % 2])
+        for bt in range(BATCH_TILES):
+            transpose_h(bt)
+            if bt > 0:
+                quantise("h", bt - 1)
+        quantise("h", BATCH_TILES - 1)
         for m in range(4):
-            make_r(m)
-        for turn in range(last):
-            if turn in (1, 3, 5):
-                make_r(4 + turn // 2)
-            make_rh(turn, whole)
-            if turn > 0:
-                make_n(turn - 1, whole)
-            blended = {3: (0, 1), 5: (2, 3), 6: (4,)}.get(turn, ())
-            for m in blended:
-                blend(m, all_tiles)(nc.gpsimd)
-        halves = [range(0, BATCH_TILES // 2), range(BATCH_TILES // 2, BATCH_TILES)]
-        make_r(last)
-        make_n(last - 1, whole)
-        make_rh(last, whole)
-        blend(last - 2, all_tiles)(nc.gpsimd)
-        for tiles in halves:
-            make_n(last, slice(P * tiles.start, P * tiles.stop))
-        blend(last - 1, all_tiles)(nc.gpsimd)
-        finishes = [blend(last, tiles) for tiles in halves]
-        for finish in finishes:
-            finish(nc.vector)
+            make_x_in(m)
+        for half in range(HALVES):
+            spread_bias_z(half)
+        for bt in range(BATCH_TILES):
+            make_z(bt)
+        bias_bank = psum.tile([P, 4 * FEATURE_TILES], F32, name="bias_bank", tag="bank")
+        nc.tensor.matmul(
+            bias_bank[:], lhsT=bias_n_rows[:], rhs=ident_bf16[:, 0 : 4 * FEATURE_TILES], start=True, stop=True
+        )
+        bias_cols = keep.tile([P, 4 * FEATURE_TILES], F32, name="bias_cols")
+        nc.vector.tensor_copy(out=bias_cols[:], in_=bias_bank[:])
+        bias_r = keep.tile([P, FEATURE_TILES], F32, name="bias_r")
+        nc.vector.tensor_tensor(
+            out=bias_r[:], in0=bias_cols[:, 0:FEATURE_TILES], in1=bias_cols[:, FEATURE_TILES : 2 * FEATURE_TILES], op=ALU.add
+        )
+        bias_hn = bias_cols[:, 2 * FEATURE_TILES : 3 * FEATURE_TILES]
+        bias_in = bias_cols[:, 3 * FEATURE_TILES : 4 * FEATURE_TILES]
+
+        def half_rows(part):
+            return slice(256 * part, 256 * (part + 1))
+        TB = {}
+        FIN = {}
+        make_r(0)
+        make_r(1)
+        make_rh(0, whole)
+        make_z(4)
+        make_n(0, whole, nc.vector)
+        make_r(2)
+        make_rh(1, whole)
+        make_z(5)
+        make_z(6)
+        make_n(1, whole, nc.vector)
+        make_r(3)
+        make_rh(2, whole)
+        make_z(7)
+        make_n(2, whole, nc.vector)
+        make_r(4)
+        make_rh(3, whole)
+        make_n(3, whole, nc.vector)
+        make_r(5)
+        make_rh(4, whole)
+        TB[0] = turn_n(0, all_tiles)
+        TB[1] = turn_n(1, all_tiles)
+        blend(0, all_tiles, TB[0])(nc.gpsimd)
+        blend(1, all_tiles, TB[1])(nc.gpsimd)
+        make_r(6)
+        make_n(4, whole, nc.vector)
+        make_rh(5, whole)
+        TB[2] = turn_n(2, all_tiles)
+        TB[3] = turn_n(3, all_tiles)
+        blend(2, all_tiles, TB[2])(nc.gpsimd)
+        blend(3, all_tiles, TB[3])(nc.gpsimd)
+        make_r(7)
+        make_n(5, whole, nc.vector)
+        make_rh(6, whole)
+        TB[4] = turn_n(4, all_tiles)
+        blend(4, all_tiles, TB[4])(nc.gpsimd)
+        make_n(6, whole, nc.vector)
+        make_rh(7, whole)
+        TB[5] = turn_n(5, all_tiles)
+        blend(5, all_tiles, TB[5])(nc.gpsimd)
+        make_n(7, half_rows(0), nc.vector)
+        make_n(7, half_rows(1), nc.vector)
+        TB[6] = turn_n(6, all_tiles)
+        TB[70] = turn_n(7, range(2 * 0, 2 * 0 + 2))
+        TB[71] = turn_n(7, range(2 * 1, 2 * 1 + 2))
+        blend(6, all_tiles, TB[6])(nc.gpsimd)
+        FIN[70] = blend(7, range(2 * 0, 2 * 0 + 2), TB[70])
+        FIN[71] = blend(7, range(2 * 1, 2 * 1 + 2), TB[71])
+        FIN[70](nc.vector)
+        FIN[71](nc.vector)

@@ -125,24 +125,29 @@ def tile_gru_kernel(
                     in_=dram_scales[name][:, 4 * quadrant : 4 * quadrant + 4, :].bitcast(I32),
                 )
 
-        for index, name in enumerate(("Wir", "Whr", "Whn", "Win")):
-            nc.gpsimd.dma_start(
-                out=bias_n_rows[FEATURE_TILES * index : FEATURE_TILES * (index + 1), :],
-                in_=dram_bias[name].rearrange("(m j) -> m j", j=P),
-            )
-        for row, name in enumerate(("Wiz", "Whz")):
-            nc.gpsimd.dma_start(out=bias_z_rows[row : row + 1, :], in_=dram_bias[name].rearrange("(o n) -> o n", o=1))
+        def load_bias_z():
+            for row, name in enumerate(("Wiz", "Whz")):
+                nc.sync.dma_start(out=bias_z_rows[row : row + 1, :], in_=dram_bias[name].rearrange("(o n) -> o n", o=1))
+
+        def load_bias_n(queue):
+            for index, name in enumerate(("Wir", "Whr", "Whn", "Win")):
+                queue.dma_start(
+                    out=bias_n_rows[FEATURE_TILES * index : FEATURE_TILES * (index + 1), :],
+                    in_=dram_bias[name].rearrange("(m j) -> m j", j=P),
+                )
 
         load_rows("x", 0, 1)
+        load_bias_z()
         load_rows("x", 1, 2)
         load_rows("x", 2, 4)
-        load_scales("Wiz")
         load_words("Wiz", 0)
+        load_scales("Wiz")
         load_rows("h", 0, 2)
         load_rows("h", 2, 4)
         for name in ("Win", "Whz", "Wir", "Whr", "Whn"):
             load_words(name, 0)
             load_scales(name)
+        load_bias_n(nc.gpsimd)
         for name in ("Wiz", "Whz", "Wir", "Whr", "Whn", "Win"):
             load_words(name, 1)
 
@@ -201,10 +206,11 @@ def tile_gru_kernel(
         z_banks = {}
 
         def spread_bias_z(half):
-            cols = slice(HALF * half, HALF * (half + 1))
             bank = psum.tile([P, HALF], F32, name="bias_z_bank", tag="bank")
-            nc.tensor.matmul(bank[:], lhsT=add_rows[:], rhs=bias_z_rows[:, cols], start=True, stop=True)
-            nc.scalar.copy(out=bias_z[:, cols], in_=bank[:])
+            nc.tensor.matmul(
+                bank[:], lhsT=add_rows[:], rhs=bias_z_rows[:, HALF * half : HALF * (half + 1)], start=True, stop=True
+            )
+            return bank
 
         def z_passes(act, name, half, bt):
             if act == "x":
@@ -332,9 +338,11 @@ def tile_gru_kernel(
             for g in range(PASSES):
                 transpose_x(bt, g, copies[g])
             if bt == 1:
-                keep_clock(2)
+                bias_banks = [spread_bias_z(half) for half in range(HALVES)]
             if bt > 0:
                 quantise("x", bt - 1)
+        for half, bank in enumerate(bias_banks):
+            nc.scalar.copy(out=bias_z[:, HALF * half : HALF * (half + 1)], in_=bank[:])
         quantise("x", BATCH_TILES - 1)
         for bt in range(BATCH_TILES):
             z_passes("x", "Wiz", 0, bt)
@@ -347,8 +355,6 @@ def tile_gru_kernel(
         quantise("h", BATCH_TILES - 1)
         for m in range(4):
             make_x_in(m)
-        for half in range(HALVES):
-            spread_bias_z(half)
         for bt in range(BATCH_TILES):
             make_z(bt)
         bias_bank = psum.tile([P, 4 * FEATURE_TILES], F32, name="bias_bank", tag="bank")
@@ -371,15 +377,15 @@ def tile_gru_kernel(
         make_r(0)
         make_r(1)
         make_rh(0, whole)
-        make_z(4)
-        make_n(0, whole, nc.vector)
         make_r(2)
         make_rh(1, whole)
+        make_n(0, whole, nc.vector)
+        make_z(4)
         make_z(5)
-        make_z(6)
         make_n(1, whole, nc.vector)
         make_r(3)
         make_rh(2, whole)
+        make_z(6)
         make_z(7)
         make_n(2, whole, nc.vector)
         make_r(4)
@@ -398,9 +404,9 @@ def tile_gru_kernel(
         TB[3] = turn_n(3, all_tiles)
         blend(2, all_tiles, TB[2])(nc.gpsimd)
         blend(3, all_tiles, TB[3])(nc.gpsimd)
-        make_r(7)
         make_n(5, whole, nc.vector)
         make_rh(6, whole)
+        make_r(7)
         TB[4] = turn_n(4, all_tiles)
         blend(4, all_tiles, TB[4])(nc.gpsimd)
         make_n(6, whole, nc.vector)

@@ -1,3 +1,4 @@
+import functools
 from contextlib import ExitStack
 
 import concourse.mybir as mybir
@@ -63,8 +64,12 @@ def tile_gru_kernel(
         results = stack.enter_context(tc.tile_pool(name="results", bufs=8))
         psum = stack.enter_context(tc.psum_pool(name="psum", bufs=8))
 
+        bias_z_rows = keep.tile([P, FEATURES], BF16, name="bias_z_rows", align_bytes=256)
+        nc.gpsimd.memset(bias_z_rows[:].bitcast(I32), 0)
         ident_f32 = keep.tile([P, P], F32, name="ident_f32", align_bytes=256)
         make_identity(nc, ident_f32[:])
+        bias_n_rows = keep.tile([P, P], BF16, name="bias_n_rows", align_bytes=256)
+        nc.gpsimd.memset(bias_n_rows[:].bitcast(I32), 0)
 
         zeros = keep.tile([P, HALF], BF16, name="zeros", align_bytes=256)
         nc.vector.memset(zeros[:].bitcast(I32), 0)
@@ -79,10 +84,6 @@ def tile_gru_kernel(
         warm_col = keep.tile([P, 1], F32, name="warm_col")
         nc.scalar.activation(out=warm_col[:], in_=zero_col[:], func=ACT.Sigmoid)
 
-        bias_z_rows = keep.tile([P, FEATURES], BF16, name="bias_z_rows", align_bytes=256)
-        nc.vector.memset(bias_z_rows[:].bitcast(I32), 0)
-        bias_n_rows = keep.tile([P, P], BF16, name="bias_n_rows", align_bytes=256)
-        nc.vector.memset(bias_n_rows[:].bitcast(I32), 0)
         planes = {}
 
         def clear_planes(name):
@@ -90,15 +91,13 @@ def tile_gru_kernel(
             nc.vector.memset(planes[name][:].bitcast(I32), 0)
 
         clear_planes("Wiz")
-        clear_planes("Win")
-        clear_planes("Whz")
         add_rows = keep.tile([P, P], BF16, name="add_rows", align_bytes=256)
         nc.vector.memset(add_rows[:], 0.0)
         nc.vector.memset(add_rows[0:2, :], 1.0)
+        for name in ("Win", "Whz", "Wir", "Whr", "Whn"):
+            clear_planes(name)
         ident_bf16 = keep.tile([P, P], BF16, name="ident_bf16", align_bytes=256)
         nc.vector.tensor_copy(out=ident_bf16[:], in_=ident_f32[:])
-        for name in ("Wir", "Whr", "Whn"):
-            clear_planes(name)
 
         rows = {}
         for act in ("x", "h"):
@@ -110,20 +109,20 @@ def tile_gru_kernel(
 
         words = {}
 
-        def load_words(name, half):
-            words[name, half] = keep.tile([P, PASSES, HALF], I32, name="words_%s_%d" % (name, half), align_bytes=256)
+        def load_words(name, half, passes=range(PASSES)):
+            if (name, half) not in words:
+                words[name, half] = keep.tile([P, PASSES, HALF], I32, name="words_%s_%d" % (name, half), align_bytes=256)
             source = dram_words[name].rearrange("g p n t -> p g (n t)")
             nc.sync.dma_start(
-                out=words[name, half][:],
-                in_=source[:, :, 4 * HALF * half : 4 * HALF * (half + 1)].bitcast(I32),
+                out=words[name, half][:, passes.start : passes.stop, :],
+                in_=source[:, passes.start : passes.stop, 4 * HALF * half : 4 * HALF * (half + 1)].bitcast(I32),
             )
 
-        def load_scales(name):
-            for quadrant in range(4):
-                nc.sync.dma_start(
-                    out=planes[name][32 * quadrant : 32 * quadrant + 4 * PASSES, :].bitcast(I32),
-                    in_=dram_scales[name][:, 4 * quadrant : 4 * quadrant + 4, :].bitcast(I32),
-                )
+        def load_scales(name, quadrant):
+            nc.sync.dma_start(
+                out=planes[name][32 * quadrant : 32 * quadrant + 4 * PASSES, :].bitcast(I32),
+                in_=dram_scales[name][:, 4 * quadrant : 4 * quadrant + 4, :].bitcast(I32),
+            )
 
         def load_bias_z():
             for row, name in enumerate(("Wiz", "Whz")):
@@ -136,17 +135,22 @@ def tile_gru_kernel(
                     in_=dram_bias[name].rearrange("(m j) -> m j", j=P),
                 )
 
+        def load_all_scales(name):
+            for quadrant in range(4):
+                load_scales(name, quadrant)
+
         load_rows("x", 0, 1)
         load_bias_z()
         load_rows("x", 1, 2)
         load_rows("x", 2, 4)
-        load_words("Wiz", 0)
-        load_scales("Wiz")
+        load_words("Wiz", 0, range(0, 1))
+        load_all_scales("Wiz")
+        load_words("Wiz", 0, range(1, 2))
         load_rows("h", 0, 2)
         load_rows("h", 2, 4)
         for name in ("Win", "Whz", "Wir", "Whr", "Whn"):
             load_words(name, 0)
-            load_scales(name)
+            load_all_scales(name)
         load_bias_n(nc.gpsimd)
         for name in ("Wiz", "Whz", "Wir", "Whr", "Whn", "Win"):
             load_words(name, 1)
@@ -212,11 +216,11 @@ def tile_gru_kernel(
             )
             return bank
 
-        def z_passes(act, name, half, bt):
-            if act == "x":
+        def z_passes(act, name, half, bt, passes=range(PASSES)):
+            if act == "x" and passes.start == 0:
                 z_banks[half, bt] = psum.tile([P, HALF], F32, name="bank_z", tag="bank")
             batch_rows = slice(P * bt, P * (bt + 1))
-            for g in range(PASSES):
+            for g in passes:
                 nc.tensor.matmul_mx(
                     out=z_banks[half, bt][:],
                     lhsT=codes[act][:, g, batch_rows].bitcast(FP8X4),
@@ -334,20 +338,28 @@ def tile_gru_kernel(
 
         copies = (nc.vector.tensor_copy, nc.scalar.copy)
         keep_clock(4)
-        for bt in range(BATCH_TILES):
+        for bt in (0, 1):
             for g in range(PASSES):
                 transpose_x(bt, g, copies[g])
-            if bt == 1:
-                bias_banks = [spread_bias_z(half) for half in range(HALVES)]
-            if bt > 0:
-                quantise("x", bt - 1)
-        for half, bank in enumerate(bias_banks):
-            nc.scalar.copy(out=bias_z[:, HALF * half : HALF * (half + 1)], in_=bank[:])
-        quantise("x", BATCH_TILES - 1)
-        for bt in range(BATCH_TILES):
+        bias_banks = [spread_bias_z(half) for half in range(HALVES)]
+        for bt in (0, 1):
+            quantise("x", bt)
+        for bt in (2, 3):
+            for g in range(PASSES):
+                transpose_x(bt, g, copies[1 if bt == 3 else g])
+        for bt in (2, 3):
+            quantise("x", bt)
+        for g in range(PASSES):
+            for bt in (0, 1):
+                z_passes("x", "Wiz", 0, bt, range(g, g + 1))
+        for bt in (2, 3):
             z_passes("x", "Wiz", 0, bt)
-        for bt in range(BATCH_TILES):
-            sort_hidden(bt, copies[(bt + 1) % 2])
+        sort_hidden(0, nc.scalar.copy)
+        sort_hidden(1, nc.vector.tensor_copy)
+        for half, bank in enumerate(bias_banks):
+            copies[half](out=bias_z[:, HALF * half : HALF * (half + 1)], in_=bank[:])
+        for bt in (2, 3):
+            sort_hidden(bt, nc.vector.tensor_copy)
         for bt in range(BATCH_TILES):
             transpose_h(bt)
             if bt > 0:
@@ -374,6 +386,8 @@ def tile_gru_kernel(
             return slice(256 * part, 256 * (part + 1))
         TB = {}
         FIN = {}
+        open_r(0)
+        open_r(1)
         make_r(0)
         make_r(1)
         make_rh(0, whole)

@@ -143,16 +143,24 @@ def tile_gru_kernel(
         load_bias_z()
         load_rows("x", 1, 2)
         load_rows("x", 2, 4)
-        load_words("Wiz", 0, range(0, 1))
         load_all_scales("Wiz")
-        load_words("Wiz", 0, range(1, 2))
+        load_words("Wiz", 0)
         load_rows("h", 0, 2)
         load_rows("h", 2, 4)
-        for name in ("Win", "Whz", "Wir", "Whr", "Whn"):
-            load_words(name, 0)
-            load_all_scales(name)
+        load_words("Wiz", 1)
+        load_all_scales("Whz")
+        load_words("Whz", 0)
+        load_words("Whz", 1)
+        load_all_scales("Wir")
+        load_words("Wir", 0)
+        load_all_scales("Whr")
+        load_words("Whr", 0)
+        load_all_scales("Whn")
+        load_words("Whn", 0)
+        load_all_scales("Win")
+        load_words("Win", 0)
         load_bias_n(nc.gpsimd)
-        for name in ("Wiz", "Whz", "Wir", "Whr", "Whn", "Win"):
+        for name in ("Wir", "Whr", "Whn", "Win"):
             load_words(name, 1)
 
         grouped = {}
@@ -337,7 +345,7 @@ def tile_gru_kernel(
             finish_z(half, bt, nc.gpsimd)
 
         copies = (nc.vector.tensor_copy, nc.scalar.copy)
-        keep_clock(4)
+        keep_clock(5)
         for bt in (0, 1):
             for g in range(PASSES):
                 transpose_x(bt, g, copies[g])
@@ -349,10 +357,7 @@ def tile_gru_kernel(
                 transpose_x(bt, g, copies[1 if bt == 3 else g])
         for bt in (2, 3):
             quantise("x", bt)
-        for g in range(PASSES):
-            for bt in (0, 1):
-                z_passes("x", "Wiz", 0, bt, range(g, g + 1))
-        for bt in (2, 3):
+        for bt in range(3):
             z_passes("x", "Wiz", 0, bt)
         sort_hidden(0, nc.scalar.copy)
         sort_hidden(1, nc.vector.tensor_copy)
@@ -361,12 +366,14 @@ def tile_gru_kernel(
         for bt in (2, 3):
             sort_hidden(bt, nc.vector.tensor_copy)
         for bt in range(BATCH_TILES):
+            if bt == 2:
+                z_passes("x", "Wiz", 0, 3)
             transpose_h(bt)
             if bt > 0:
                 quantise("h", bt - 1)
         quantise("h", BATCH_TILES - 1)
-        for m in range(4):
-            make_x_in(m)
+        for bt in (0, 1):
+            z_passes("x", "Wiz", 1, bt)
         for bt in range(BATCH_TILES):
             make_z(bt)
         bias_bank = psum.tile([P, 4 * FEATURE_TILES], F32, name="bias_bank", tag="bank")
@@ -386,29 +393,27 @@ def tile_gru_kernel(
             return slice(256 * part, 256 * (part + 1))
         TB = {}
         FIN = {}
-        open_r(0)
-        open_r(1)
-        make_r(0)
-        make_r(1)
-        make_rh(0, whole)
-        make_r(2)
-        make_rh(1, whole)
-        make_n(0, whole, nc.vector)
         make_z(4)
         make_z(5)
-        make_n(1, whole, nc.vector)
-        make_r(3)
-        make_rh(2, whole)
         make_z(6)
         make_z(7)
-        make_n(2, whole, nc.vector)
+        make_r(0)
+        make_r(1)
+        make_r(2)
+        make_r(3)
+        make_rh(0, whole)
+        make_rh(1, whole)
+        make_n(0, whole, nc.vector)
         make_r(4)
+        make_rh(2, whole)
+        make_n(1, whole, nc.vector)
         make_rh(3, whole)
-        make_n(3, whole, nc.vector)
+        make_n(2, whole, nc.vector)
         make_r(5)
-        make_rh(4, whole)
         TB[0] = turn_n(0, all_tiles)
         TB[1] = turn_n(1, all_tiles)
+        make_rh(4, whole)
+        make_n(3, whole, nc.vector)
         blend(0, all_tiles, TB[0])(nc.gpsimd)
         blend(1, all_tiles, TB[1])(nc.gpsimd)
         make_r(6)

@@ -109,14 +109,16 @@ def tile_gru_kernel(
 
         words = {}
 
-        def load_words(name, half, passes=range(PASSES)):
-            if (name, half) not in words:
-                words[name, half] = keep.tile([P, PASSES, HALF], I32, name="words_%s_%d" % (name, half), align_bytes=256)
+        def load_words(name, first, last):
+            tile = keep.tile([P, PASSES, HALF * (last - first)], I32, name="words_%s_%d" % (name, first), align_bytes=256)
+            for half in range(first, last):
+                words[name, half] = tile, HALF * (half - first)
             source = dram_words[name].rearrange("g p n t -> p g (n t)")
-            nc.sync.dma_start(
-                out=words[name, half][:, passes.start : passes.stop, :],
-                in_=source[:, passes.start : passes.stop, 4 * HALF * half : 4 * HALF * (half + 1)].bitcast(I32),
-            )
+            nc.sync.dma_start(out=tile[:], in_=source[:, :, 4 * HALF * first : 4 * HALF * last].bitcast(I32))
+
+        def word_columns(name, g, first, width):
+            tile, start = words[name, first // HALF]
+            return tile[:, g, start + first % HALF : start + first % HALF + width].bitcast(FP8X4)
 
         def load_scales(name, quadrant):
             nc.sync.dma_start(
@@ -144,24 +146,19 @@ def tile_gru_kernel(
         load_rows("x", 1, 2)
         load_rows("x", 2, 4)
         load_all_scales("Wiz")
-        load_words("Wiz", 0)
+        load_words("Wiz", 0, 1)
         load_rows("h", 0, 2)
         load_rows("h", 2, 4)
-        load_words("Wiz", 1)
+        load_words("Wiz", 1, 2)
         load_all_scales("Whz")
-        load_words("Whz", 0)
-        load_words("Whz", 1)
-        load_all_scales("Wir")
-        load_words("Wir", 0)
-        load_all_scales("Whr")
-        load_words("Whr", 0)
-        load_all_scales("Whn")
-        load_words("Whn", 0)
-        load_all_scales("Win")
-        load_words("Win", 0)
+        load_words("Whz", 0, 1)
+        load_words("Whz", 1, 2)
         load_bias_n(nc.gpsimd)
         for name in ("Wir", "Whr", "Whn", "Win"):
-            load_words(name, 1)
+            load_all_scales(name)
+            load_words(name, 0, 1)
+        for name in ("Wir", "Whr", "Whn", "Win"):
+            load_words(name, 1, 2)
 
         grouped = {}
         codes = {}
@@ -233,7 +230,7 @@ def tile_gru_kernel(
                     out=z_banks[half, bt][:],
                     lhsT=codes[act][:, g, batch_rows].bitcast(FP8X4),
                     lhsT_scale=act_planes[act][:, g, batch_rows],
-                    rhs=words[name, half][:, g, :].bitcast(FP8X4),
+                    rhs=word_columns(name, g, HALF * half, HALF),
                     rhs_scale=planes[name][4 * g : P, HALF * half : HALF * (half + 1)],
                     start=(act == "x" and g == 0),
                     stop=(act == "h" and g == PASSES - 1),
@@ -252,10 +249,9 @@ def tile_gru_kernel(
             multiplier.tensor_tensor(out=zh[:, bt, cols], in0=z[:, bt, cols], in1=rows["h"][:, bt, cols], op=ALU.mult)
 
         def one_pass(bank, act, name, m, batch, g, start, stop):
-            half, tile_in_half = divmod(m, HALF // P)
             nc.tensor.matmul_mx(
                 out=bank[:],
-                lhsT=words[name, half][:, g, P * tile_in_half : P * (tile_in_half + 1)].bitcast(FP8X4),
+                lhsT=word_columns(name, g, P * m, P),
                 lhsT_scale=planes[name][4 * g : P, P * m : P * (m + 1)],
                 rhs=codes[act][:, g, batch].bitcast(FP8X4),
                 rhs_scale=act_planes[act][:, g, batch],
@@ -355,6 +351,7 @@ def tile_gru_kernel(
         for bt in (2, 3):
             for g in range(PASSES):
                 transpose_x(bt, g, copies[1 if bt == 3 else g])
+        keep_clock(2)
         for bt in (2, 3):
             quantise("x", bt)
         for bt in range(3):
@@ -376,18 +373,20 @@ def tile_gru_kernel(
             z_passes("x", "Wiz", 1, bt)
         for bt in range(BATCH_TILES):
             make_z(bt)
-        bias_bank = psum.tile([P, 4 * FEATURE_TILES], F32, name="bias_bank", tag="bank")
-        nc.tensor.matmul(
-            bias_bank[:], lhsT=bias_n_rows[:], rhs=ident_bf16[:, 0 : 4 * FEATURE_TILES], start=True, stop=True
-        )
-        bias_cols = keep.tile([P, 4 * FEATURE_TILES], F32, name="bias_cols")
+        bias_bank = psum.tile([P, 3 * FEATURE_TILES], F32, name="bias_bank", tag="bank")
+        for place, first_row, start, stop in ((0, 0, True, False), (0, 1, False, True), (1, 2, True, True), (2, 3, True, True)):
+            nc.tensor.matmul(
+                bias_bank[:, FEATURE_TILES * place : FEATURE_TILES * (place + 1)],
+                lhsT=bias_n_rows[:],
+                rhs=ident_bf16[:, FEATURE_TILES * first_row : FEATURE_TILES * (first_row + 1)],
+                start=start,
+                stop=stop,
+            )
+        bias_cols = keep.tile([P, 3 * FEATURE_TILES], F32, name="bias_cols")
         nc.vector.tensor_copy(out=bias_cols[:], in_=bias_bank[:])
-        bias_r = keep.tile([P, FEATURE_TILES], F32, name="bias_r")
-        nc.vector.tensor_tensor(
-            out=bias_r[:], in0=bias_cols[:, 0:FEATURE_TILES], in1=bias_cols[:, FEATURE_TILES : 2 * FEATURE_TILES], op=ALU.add
-        )
-        bias_hn = bias_cols[:, 2 * FEATURE_TILES : 3 * FEATURE_TILES]
-        bias_in = bias_cols[:, 3 * FEATURE_TILES : 4 * FEATURE_TILES]
+        bias_r = bias_cols[:, 0:FEATURE_TILES]
+        bias_hn = bias_cols[:, FEATURE_TILES : 2 * FEATURE_TILES]
+        bias_in = bias_cols[:, 2 * FEATURE_TILES : 3 * FEATURE_TILES]
 
         def half_rows(part):
             return slice(256 * part, 256 * (part + 1))
@@ -403,28 +402,28 @@ def tile_gru_kernel(
         make_r(3)
         make_rh(0, whole)
         make_rh(1, whole)
-        make_n(0, whole, nc.vector)
-        make_r(4)
         make_rh(2, whole)
-        make_n(1, whole, nc.vector)
         make_rh(3, whole)
+        make_n(0, whole, nc.vector)
+        make_n(1, whole, nc.vector)
         make_n(2, whole, nc.vector)
+        make_n(3, whole, nc.vector)
+        make_r(4)
+        make_rh(4, whole)
         make_r(5)
         TB[0] = turn_n(0, all_tiles)
         TB[1] = turn_n(1, all_tiles)
-        make_rh(4, whole)
-        make_n(3, whole, nc.vector)
         blend(0, all_tiles, TB[0])(nc.gpsimd)
         blend(1, all_tiles, TB[1])(nc.gpsimd)
-        make_r(6)
-        make_n(4, whole, nc.vector)
         make_rh(5, whole)
+        make_n(4, whole, nc.vector)
+        make_r(6)
         TB[2] = turn_n(2, all_tiles)
         TB[3] = turn_n(3, all_tiles)
         blend(2, all_tiles, TB[2])(nc.gpsimd)
         blend(3, all_tiles, TB[3])(nc.gpsimd)
-        make_n(5, whole, nc.vector)
         make_rh(6, whole)
+        make_n(5, whole, nc.vector)
         make_r(7)
         TB[4] = turn_n(4, all_tiles)
         blend(4, all_tiles, TB[4])(nc.gpsimd)
@@ -435,10 +434,10 @@ def tile_gru_kernel(
         make_n(7, half_rows(0), nc.vector)
         make_n(7, half_rows(1), nc.vector)
         TB[6] = turn_n(6, all_tiles)
+        blend(6, all_tiles, TB[6])(nc.vector)
         TB[70] = turn_n(7, range(2 * 0, 2 * 0 + 2))
-        TB[71] = turn_n(7, range(2 * 1, 2 * 1 + 2))
-        blend(6, all_tiles, TB[6])(nc.gpsimd)
         FIN[70] = blend(7, range(2 * 0, 2 * 0 + 2), TB[70])
+        TB[71] = turn_n(7, range(2 * 1, 2 * 1 + 2))
         FIN[71] = blend(7, range(2 * 1, 2 * 1 + 2), TB[71])
         FIN[70](nc.vector)
         FIN[71](nc.vector)

@@ -104,7 +104,7 @@ def tile_gru_kernel(
             rows[act] = keep.tile([P, BATCH_TILES, K], BF16, name="rows_" + act, align_bytes=256)
 
         def load_rows(act, first, last):
-            source = dram_rows[act].rearrange("(t b) k -> b t k", b=P)
+            source = dram_rows[act].rearrange("(b t) k -> b t k", b=P)
             nc.sync.dma_start(out=rows[act][:, first:last, :], in_=source[:, first:last, :])
 
         words = {}
@@ -309,7 +309,7 @@ def tile_gru_kernel(
             adder.tensor_tensor(out=n_in[:], in0=bank, in1=rh[m][:, batch], op=ALU.add)
             nc.scalar.activation(out=n[m][:, batch], in_=n_in[:], func=ACT.Tanh, bias=bias_in[:, m : m + 1])
 
-        out_view = out.rearrange("(t b) n -> b t n", b=P)
+        out_view = out.rearrange("(b t) n -> b t n", b=P)
 
         def turn_n(m, tiles):
             bank = psum.tile([P, len(tiles), P], F32, name="n_T", tag="bank")
@@ -323,10 +323,12 @@ def tile_gru_kernel(
             part = work.tile([P, len(tiles), P], F32, name="part", align_bytes=256)
             nc.vector.scalar_tensor_tensor(out=part[:], in0=z[:, span, cols], scalar=1.0, in1=bank[:], op0=ALU.subtract, op1=ALU.mult)
 
-            def finish(adder):
-                res = results.tile([P, len(tiles), P], F32, name="res", align_bytes=256)
-                adder.tensor_tensor(out=res[:], in0=zh[:, span, cols], in1=part[:], op=ALU.subtract)
-                nc.sync.dma_start(out=out_view[:, span, cols], in_=res[:])
+            def finish(adder, first=0, last=len(tiles)):
+                count = last - first
+                picked = slice(tiles.start + first, tiles.start + last)
+                res = results.tile([P, count, P], F32, name="res", align_bytes=256)
+                adder.tensor_tensor(out=res[:], in0=zh[:, picked, cols], in1=part[:, first:last, :], op=ALU.subtract)
+                nc.sync.dma_start(out=out_view[:, picked, cols], in_=res[:])
 
             return finish
 
@@ -434,7 +436,9 @@ def tile_gru_kernel(
         make_n(7, half_rows(0), nc.vector)
         make_n(7, half_rows(1), nc.vector)
         TB[6] = turn_n(6, all_tiles)
-        blend(6, all_tiles, TB[6])(nc.vector)
+        FIN[6] = blend(6, all_tiles, TB[6])
+        FIN[6](nc.vector, 0, 2)
+        FIN[6](nc.gpsimd, 2, 4)
         TB[70] = turn_n(7, range(2 * 0, 2 * 0 + 2))
         FIN[70] = blend(7, range(2 * 0, 2 * 0 + 2), TB[70])
         TB[71] = turn_n(7, range(2 * 1, 2 * 1 + 2))

import functools
from contextlib import ExitStack

import concourse.mybir as mybir
from concourse.masks import make_identity

F32 = mybir.dt.float32
BF16 = mybir.dt.bfloat16
I32 = mybir.dt.int32
U32 = mybir.dt.uint32
U8 = mybir.dt.uint8
FP8X4 = mybir.dt.float8_e4m3fn_x4
ACT = mybir.ActivationFunctionType
ALU = mybir.AluOpType

P = 128
BATCH = 512
K = 1024
FEATURES = 1024
K_PASS = 4 * P
PASSES = K // K_PASS
BATCH_TILES = BATCH // P
FEATURE_TILES = FEATURES // P
HALF = 512
HALVES = FEATURES // HALF

FLOPS = 2 * BATCH * K * FEATURES * 6


def tile_gru_kernel(
    tc,
    x,
    hidden,
    Wir_w_words,
    Wir_w_scales,
    Wir_b,
    Whr_w_words,
    Whr_w_scales,
    Whr_b,
    Wiz_w_words,
    Wiz_w_scales,
    Wiz_b,
    Whz_w_words,
    Whz_w_scales,
    Whz_b,
    Win_w_words,
    Win_w_scales,
    Win_b,
    Whn_w_words,
    Whn_w_scales,
    Whn_b,
    out,
):
    nc = tc.nc
    dram_words = {"Wir": Wir_w_words, "Whr": Whr_w_words, "Wiz": Wiz_w_words, "Whz": Whz_w_words, "Win": Win_w_words, "Whn": Whn_w_words}
    dram_scales = {"Wir": Wir_w_scales, "Whr": Whr_w_scales, "Wiz": Wiz_w_scales, "Whz": Whz_w_scales, "Win": Win_w_scales, "Whn": Whn_w_scales}
    dram_bias = {"Wir": Wir_b, "Whr": Whr_b, "Wiz": Wiz_b, "Whz": Whz_b, "Win": Win_b, "Whn": Whn_b}
    dram_rows = {"x": x, "h": hidden}

    with ExitStack() as stack:
        stack.enter_context(tc.manual_schedule())
        keep = stack.enter_context(tc.tile_pool(name="keep", bufs=1))
        work = stack.enter_context(tc.tile_pool(name="work", bufs=4))
        results = stack.enter_context(tc.tile_pool(name="results", bufs=8))
        psum = stack.enter_context(tc.psum_pool(name="psum", bufs=8))

        bias_z_rows = keep.tile([P, FEATURES], BF16, name="bias_z_rows", align_bytes=256)
        nc.gpsimd.memset(bias_z_rows[:].bitcast(I32), 0)
        ident_f32 = keep.tile([P, P], F32, name="ident_f32", align_bytes=256)
        make_identity(nc, ident_f32[:])
        bias_n_rows = keep.tile([P, P], BF16, name="bias_n_rows", align_bytes=256)
        nc.gpsimd.memset(bias_n_rows[:].bitcast(I32), 0)

        zeros = keep.tile([P, HALF], BF16, name="zeros", align_bytes=256)
        nc.vector.memset(zeros[:].bitcast(I32), 0)

        def keep_clock(count):
            idle_bank = psum.tile([P, HALF], F32, name="idle_bank", tag="bank")
            for turn in range(count):
                nc.tensor.matmul(idle_bank[:], lhsT=zeros[:, 0:P], rhs=zeros[:], start=True, stop=True)

        zero_col = keep.tile([P, 1], F32, name="zero_col")
        nc.vector.memset(zero_col[:], 0.0)
        warm_col = keep.tile([P, 1], F32, name="warm_col")
        nc.scalar.activation(out=warm_col[:], in_=zero_col[:], func=ACT.Sigmoid)

        planes = {}

        def clear_planes(name):
            planes[name] = keep.tile([P, FEATURES], U8, name="planes_" + name, align_bytes=256)
            nc.vector.memset(planes[name][:].bitcast(I32), 0)

        clear_planes("Wiz")
        add_rows = keep.tile([P, P], BF16, name="add_rows", align_bytes=256)
        nc.vector.memset(add_rows[:], 0.0)
        nc.vector.memset(add_rows[0:2, :], 1.0)
        for name in ("Win", "Whz", "Wir", "Whr", "Whn"):
            clear_planes(name)
        ident_bf16 = keep.tile([P, P], BF16, name="ident_bf16", align_bytes=256)
        nc.vector.tensor_copy(out=ident_bf16[:], in_=ident_f32[:])

        rows = {}
        for act in ("x", "h"):
            rows[act] = keep.tile([P, BATCH_TILES, K], BF16, name="rows_" + act, align_bytes=256)

        def load_rows(act, first, last):
            source = dram_rows[act].rearrange("(b t) k -> b t k", b=P)
            nc.sync.dma_start(out=rows[act][:, first:last, :], in_=source[:, first:last, :])

        words = {}

        def load_words(name, first, last):
            tile = keep.tile([P, PASSES, HALF * (last - first)], I32, name="words_%s_%d" % (name, first), align_bytes=256)
            for half in range(first, last):
                words[name, half] = tile, HALF * (half - first)
            source = dram_words[name].rearrange("g p n t -> p g (n t)")
            nc.sync.dma_start(out=tile[:], in_=source[:, :, 4 * HALF * first : 4 * HALF * last].bitcast(I32))

        def word_columns(name, g, first, width):
            tile, start = words[name, first // HALF]
            return tile[:, g, start + first % HALF : start + first % HALF + width].bitcast(FP8X4)

        def load_scales(name, quadrant):
            nc.sync.dma_start(
                out=planes[name][32 * quadrant : 32 * quadrant + 4 * PASSES, :].bitcast(I32),
                in_=dram_scales[name][:, 4 * quadrant : 4 * quadrant + 4, :].bitcast(I32),
            )

        def load_bias_z():
            for row, name in enumerate(("Wiz", "Whz")):
                nc.sync.dma_start(out=bias_z_rows[row : row + 1, :], in_=dram_bias[name].rearrange("(o n) -> o n", o=1))

        def load_bias_n(queue):
            for index, name in enumerate(("Wir", "Whr", "Whn", "Win")):
                queue.dma_start(
                    out=bias_n_rows[FEATURE_TILES * index : FEATURE_TILES * (index + 1), :],
                    in_=dram_bias[name].rearrange("(m j) -> m j", j=P),
                )

        def load_all_scales(name):
            for quadrant in range(4):
                load_scales(name, quadrant)

        load_rows("x", 0, 1)
        load_bias_z()
        load_rows("x", 1, 2)
        load_rows("x", 2, 4)
        load_all_scales("Wiz")
        load_words("Wiz", 0, 1)
        load_rows("h", 0, 2)
        load_rows("h", 2, 4)
        load_words("Wiz", 1, 2)
        load_all_scales("Whz")
        load_words("Whz", 0, 1)
        load_words("Whz", 1, 2)
        load_bias_n(nc.gpsimd)
        for name in ("Wir", "Whr", "Whn", "Win"):
            load_all_scales(name)
            load_words(name, 0, 1)
        for name in ("Wir", "Whr", "Whn", "Win"):
            load_words(name, 1, 2)

        grouped = {}
        codes = {}
        act_planes = {}
        for act in ("x", "h"):
            for bt in range(BATCH_TILES):
                grouped[act, bt] = keep.tile([P, PASSES, 4 * P], BF16, name="grouped_%s_%d" % (act, bt), align_bytes=256)
            codes[act] = keep.tile([P, PASSES, BATCH], U32, name="codes_" + act, align_bytes=256)
            act_planes[act] = keep.tile([P, PASSES, BATCH], U8, name="act_planes_" + act, align_bytes=256)

        sorted_h = keep.tile([P, BATCH_TILES, PASSES, 2, P], F32, name="sorted_h", align_bytes=256)

        def sort_hidden(bt, copy):
            copy(
                out=sorted_h[:, bt, :, :, :],
                in_=rows["h"][:, bt, :].bitcast(F32).rearrange("b (g p u) -> b g u p", g=PASSES, u=2),
            )

        def transpose_x(bt, g, copy):
            bank = psum.tile([P, 2, P], F32, name="x_T", tag="bank")
            for u in range(2):
                source = rows["x"][:, bt, :].bitcast(F32)[:, 256 * g + u : 256 * (g + 1) : 2]
                nc.tensor.transpose(bank[:, u, :], source, ident_f32[:])
            copy(
                out=grouped["x", bt][:, g, :].bitcast(F32).rearrange("p (b u) -> p b u", u=2),
                in_=bank[:].rearrange("p u b -> p b u"),
            )

        def transpose_h(bt):
            bank = psum.tile([P, PASSES, 2, P], F32, name="h_T", tag="bank")
            for g in range(PASSES):
                for u in range(2):
                    nc.tensor.transpose(bank[:, g, u, :], sorted_h[:, bt, g, u, :], ident_f32[:])
            copy = nc.scalar.copy if bt % 2 else nc.vector.tensor_copy
            copy(
                out=grouped["h", bt][:].bitcast(F32).rearrange("p g (b u) -> p g b u", u=2),
                in_=bank[:].rearrange("p g u b -> p g b u"),
            )

        def quantise_pass(act, bt, g):
            nc.vector.quantize_mx(
                out=codes[act][:, g, P * bt : P * (bt + 1)].bitcast(FP8X4),
                scales=act_planes[act][:, g, P * bt : P * (bt + 1)],
                in_=grouped[act, bt][:, g, :],
            )

        def quantise(act, bt):
            for g in range(PASSES):
                quantise_pass(act, bt, g)

        bias_z = keep.tile([P, FEATURES], F32, name="bias_z", align_bytes=256)
        z = keep.tile([P, BATCH_TILES, FEATURES], F32, name="z", align_bytes=256)
        zh = keep.tile([P, BATCH_TILES, FEATURES], F32, name="zh", align_bytes=256)
        z_banks = {}

        def spread_bias_z(half):
            bank = psum.tile([P, HALF], F32, name="bias_z_bank", tag="bank")
            nc.tensor.matmul(
                bank[:], lhsT=add_rows[:], rhs=bias_z_rows[:, HALF * half : HALF * (half + 1)], start=True, stop=True
            )
            return bank

        def z_passes(act, name, half, bt, passes=range(PASSES)):
            if act == "x" and passes.start == 0:
                z_banks[half, bt] = psum.tile([P, HALF], F32, name="bank_z", tag="bank")
            batch_rows = slice(P * bt, P * (bt + 1))
            for g in passes:
                nc.tensor.matmul_mx(
                    out=z_banks[half, bt][:],
                    lhsT=codes[act][:, g, batch_rows].bitcast(FP8X4),
                    lhsT_scale=act_planes[act][:, g, batch_rows],
                    rhs=word_columns(name, g, HALF * half, HALF),
                    rhs_scale=planes[name][4 * g : P, HALF * half : HALF * (half + 1)],
                    start=(act == "x" and g == 0),
                    stop=(act == "h" and g == PASSES - 1),
                )

        def finish_z(half, bt, multiplier):
            cols = slice(HALF * half, HALF * (half + 1))
            z_in = work.tile([P, HALF], F32, name="z_in", align_bytes=256)
            nc.vector.tensor_tensor(out=z_in[:], in0=z_banks[half, bt][:], in1=bias_z[:, cols], op=ALU.add)
            nc.scalar.activation(out=z[:, bt, cols], in_=z_in[:], func=ACT.Sigmoid)
            if multiplier is not None:
                z_times_hidden(half, bt, multiplier)

        def z_times_hidden(half, bt, multiplier):
            cols = slice(HALF * half, HALF * (half + 1))
            multiplier.tensor_tensor(out=zh[:, bt, cols], in0=z[:, bt, cols], in1=rows["h"][:, bt, cols], op=ALU.mult)

        def one_pass(bank, act, name, m, batch, g, start, stop):
            nc.tensor.matmul_mx(
                out=bank[:],
                lhsT=word_columns(name, g, P * m, P),
                lhsT_scale=planes[name][4 * g : P, P * m : P * (m + 1)],
                rhs=codes[act][:, g, batch].bitcast(FP8X4),
                rhs_scale=act_planes[act][:, g, batch],
                start=start,
                stop=stop,
            )

        def passes(bank, pairs, m, batch, first=True, final=True):
            steps = [(act, name, g) for act, name in pairs for g in range(PASSES)]
            for step, (act, name, g) in enumerate(steps):
                one_pass(bank, act, name, m, batch, g, first and step == 0, final and step == len(steps) - 1)

        def product(label, pairs, m, batch):
            bank = psum.tile([P, batch.stop - batch.start], F32, name="bank_" + label, tag="bank")
            passes(bank, pairs, m, batch)
            return bank

        whole = slice(0, BATCH)
        x_in = {}

        r = {}
        rh = {}
        n = {}

        r_banks = {}

        def open_r(m):
            r_banks[m] = psum.tile([P, BATCH], F32, name="bank_r", tag="bank")
            passes(r_banks[m], (("x", "Wir"),), m, whole, final=False)

        def make_r(m):
            if m not in r_banks:
                open_r(m)
            bank = r_banks[m]
            passes(bank, (("h", "Whr"),), m, whole, first=False)
            r[m] = work.tile([P, BATCH], F32, name="r", align_bytes=256)
            nc.scalar.activation(out=r[m][:], in_=bank[:], func=ACT.Sigmoid, bias=bias_r[:, m : m + 1])
            rh[m] = work.tile([P, BATCH], F32, name="rh", align_bytes=256)
            n[m] = keep.tile([P, BATCH], F32, name="n_%d" % m, align_bytes=256)

        def make_rh(m, batch):
            bank = product("hn", (("h", "Whn"),), m, batch)
            nc.vector.scalar_tensor_tensor(
                out=rh[m][:, batch], in0=bank[:], scalar=bias_hn[:, m : m + 1], in1=r[m][:, batch], op0=ALU.add, op1=ALU.mult
            )

        def make_x_in(m):
            bank = product("x_in", (("x", "Win"),), m, whole)
            x_in[m] = keep.tile([P, BATCH], F32, name="x_in_%d" % m, align_bytes=256)
            nc.scalar.copy(out=x_in[m][:], in_=bank[:])

        def make_n(m, batch, adder):
            bank = x_in[m][:, batch] if m in x_in else product("in", (("x", "Win"),), m, batch)[:]
            n_in = work.tile([P, batch.stop - batch.start], F32, name="n_in", align_bytes=256)
            adder.tensor_tensor(out=n_in[:], in0=bank, in1=rh[m][:, batch], op=ALU.add)
            nc.scalar.activation(out=n[m][:, batch], in_=n_in[:], func=ACT.Tanh, bias=bias_in[:, m : m + 1])

        out_view = out.rearrange("(b t) n -> b t n", b=P)

        def turn_n(m, tiles):
            bank = psum.tile([P, len(tiles), P], F32, name="n_T", tag="bank")
            for index, bt in enumerate(tiles):
                nc.tensor.transpose(bank[:, index, :], n[m][:, P * bt : P * (bt + 1)], ident_f32[:])
            return bank

        def blend(m, tiles, bank):
            cols = slice(P * m, P * (m + 1))
            span = slice(tiles.start, tiles.stop)
            part = work.tile([P, len(tiles), P], F32, name="part", align_bytes=256)
            nc.vector.scalar_tensor_tensor(out=part[:], in0=z[:, span, cols], scalar=1.0, in1=bank[:], op0=ALU.subtract, op1=ALU.mult)

            def finish(adder, first=0, last=len(tiles)):
                count = last - first
                picked = slice(tiles.start + first, tiles.start + last)
                res = results.tile([P, count, P], F32, name="res", align_bytes=256)
                adder.tensor_tensor(out=res[:], in0=zh[:, picked, cols], in1=part[:, first:last, :], op=ALU.subtract)
                nc.sync.dma_start(out=out_view[:, picked, cols], in_=res[:])

            return finish

        all_tiles = range(BATCH_TILES)
        last = FEATURE_TILES - 1

        def make_z(index):
            half, bt = divmod(index, BATCH_TILES)
            if (half, bt) not in z_banks:
                z_passes("x", "Wiz", half, bt)
            z_passes("h", "Whz", half, bt)
            finish_z(half, bt, nc.gpsimd)

        copies = (nc.vector.tensor_copy, nc.scalar.copy)
        keep_clock(5)
        for bt in (0, 1):
            for g in range(PASSES):
                transpose_x(bt, g, copies[g])
        bias_banks = [spread_bias_z(half) for half in range(HALVES)]
        for bt in (0, 1):
            quantise("x", bt)
        for bt in (2, 3):
            for g in range(PASSES):
                transpose_x(bt, g, copies[1 if bt == 3 else g])
        keep_clock(2)
        for bt in (2, 3):
            quantise("x", bt)
        for bt in range(3):
            z_passes("x", "Wiz", 0, bt)
        sort_hidden(0, nc.scalar.copy)
        sort_hidden(1, nc.vector.tensor_copy)
        for half, bank in enumerate(bias_banks):
            copies[half](out=bias_z[:, HALF * half : HALF * (half + 1)], in_=bank[:])
        for bt in (2, 3):
            sort_hidden(bt, nc.vector.tensor_copy)
        for bt in range(BATCH_TILES):
            if bt == 2:
                z_passes("x", "Wiz", 0, 3)
            transpose_h(bt)
            if bt > 0:
                quantise("h", bt - 1)
        quantise("h", BATCH_TILES - 1)
        for bt in (0, 1):
            z_passes("x", "Wiz", 1, bt)
        for bt in range(BATCH_TILES):
            make_z(bt)
        bias_bank = psum.tile([P, 3 * FEATURE_TILES], F32, name="bias_bank", tag="bank")
        for place, first_row, start, stop in ((0, 0, True, False), (0, 1, False, True), (1, 2, True, True), (2, 3, True, True)):
            nc.tensor.matmul(
                bias_bank[:, FEATURE_TILES * place : FEATURE_TILES * (place + 1)],
                lhsT=bias_n_rows[:],
                rhs=ident_bf16[:, FEATURE_TILES * first_row : FEATURE_TILES * (first_row + 1)],
                start=start,
                stop=stop,
            )
        bias_cols = keep.tile([P, 3 * FEATURE_TILES], F32, name="bias_cols")
        nc.vector.tensor_copy(out=bias_cols[:], in_=bias_bank[:])
        bias_r = bias_cols[:, 0:FEATURE_TILES]
        bias_hn = bias_cols[:, FEATURE_TILES : 2 * FEATURE_TILES]
        bias_in = bias_cols[:, 2 * FEATURE_TILES : 3 * FEATURE_TILES]

        def half_rows(part):
            return slice(256 * part, 256 * (part + 1))
        TB = {}
        FIN = {}
        make_z(4)
        make_z(5)
        make_z(6)
        make_z(7)
        make_r(0)
        make_r(1)
        make_r(2)
        make_r(3)
        make_rh(0, whole)
        make_rh(1, whole)
        make_rh(2, whole)
        make_rh(3, whole)
        make_n(0, whole, nc.vector)
        make_n(1, whole, nc.vector)
        make_n(2, whole, nc.vector)
        make_n(3, whole, nc.vector)
        make_r(4)
        make_rh(4, whole)
        make_r(5)
        TB[0] = turn_n(0, all_tiles)
        TB[1] = turn_n(1, all_tiles)
        blend(0, all_tiles, TB[0])(nc.gpsimd)
        blend(1, all_tiles, TB[1])(nc.gpsimd)
        make_rh(5, whole)
        make_n(4, whole, nc.vector)
        make_r(6)
        TB[2] = turn_n(2, all_tiles)
        TB[3] = turn_n(3, all_tiles)
        blend(2, all_tiles, TB[2])(nc.gpsimd)
        blend(3, all_tiles, TB[3])(nc.gpsimd)
        make_rh(6, whole)
        make_n(5, whole, nc.vector)
        make_r(7)
        TB[4] = turn_n(4, all_tiles)
        blend(4, all_tiles, TB[4])(nc.gpsimd)
        make_n(6, whole, nc.vector)
        make_rh(7, whole)
        TB[5] = turn_n(5, all_tiles)
        blend(5, all_tiles, TB[5])(nc.gpsimd)
        make_n(7, half_rows(0), nc.vector)
        make_n(7, half_rows(1), nc.vector)
        TB[6] = turn_n(6, all_tiles)
        FIN[6] = blend(6, all_tiles, TB[6])
        FIN[6](nc.vector, 0, 2)
        FIN[6](nc.gpsimd, 2, 4)
        TB[70] = turn_n(7, range(2 * 0, 2 * 0 + 2))
        FIN[70] = blend(7, range(2 * 0, 2 * 0 + 2), TB[70])
        TB[71] = turn_n(7, range(2 * 1, 2 * 1 + 2))
        FIN[71] = blend(7, range(2 * 1, 2 * 1 + 2), TB[71])
        FIN[70](nc.vector)
        FIN[71](nc.vector)
